import numpy as np
import ml_dtypes


def mxq(x, axis, fmt="e4m3"):
    dtype, down = {"e4m3": (ml_dtypes.float8_e4m3fn, 7), "e5m2": (ml_dtypes.float8_e5m2, 14)}[fmt]
    v = np.moveaxis(np.asarray(x, np.float32).astype(ml_dtypes.bfloat16).astype(np.float64), axis, -1)
    blocks = v.reshape(v.shape[:-1] + (-1, 32))
    amax = np.abs(blocks).max(-1, keepdims=True)
    byte = np.maximum(np.where(amax > 0, np.frexp(amax)[1] - 1 + 127, 0) - down, 1)
    scale = np.exp2(byte - 127.0)
    codes = (blocks / scale).astype(np.float32).astype(dtype).astype(np.float64)
    return np.moveaxis((codes * scale).reshape(v.shape), -1, axis)


WIDE = False


def mx_kscale(k):
    if not WIDE:
        return np.ones(k)
    levels = np.array([10, -10, 5, -5, 0])
    a = np.random.permutation(np.resize(levels, k // 512 * 4)).reshape(k // 512, 4)
    idx = np.arange(k)
    return np.exp2(a[idx // 512, idx % 128 // 32])


BF16 = ml_dtypes.bfloat16


def bf(x):
    return np.asarray(x, np.float32).astype(BF16)


def f64(x):
    return np.asarray(x).astype(np.float64)


B, S, D = 2, 2048, 128


def setup_inputs():
    t = mx_kscale(S)
    q = np.random.standard_normal((B, S, D)) * 3.0 / np.sqrt(D)
    k = np.random.standard_normal((B, S, D))
    v = np.random.standard_normal((B, S, D))
    q[:, :, 0] = np.log(2.0)
    k[:, :, 0] += np.log2(t)[None, :]
    v = v * (t.mean() / t)[None, :, None]
    return {"q_scaled": bf(q), "k": bf(k), "v": bf(v),
            "mask": bf(np.random.random((B, S)) > 0.2)}


def reference(q_scaled, k, v, mask):
    qs, m = f64(q_scaled), f64(mask)
    with np.errstate(divide="ignore"):
        lm = np.log(m)
    s = qs @ f64(k).transpose(0, 2, 1) + lm[:, None, :]
    e = np.exp(s - s.max(-1, keepdims=True))
    out = (mxq(e, 2, "e4m3") @ mxq(f64(v), 1, "e4m3")) / e.sum(-1, keepdims=True)
    return out * m[..., None] + qs * (1.0 - m)[..., None]

@@ -1,0 +1,199 @@
+from contextlib import ExitStack
+
+import concourse.mybir as mybir
+from concourse.masks import make_identity
+
+BF16 = mybir.dt.bfloat16
+F32 = mybir.dt.float32
+U32 = mybir.dt.uint32
+U8 = mybir.dt.uint8
+FP8X4 = mybir.dt.float8_e4m3fn_x4
+ALU = mybir.AluOpType
+ACT = mybir.ActivationFunctionType
+AX = mybir.AxisListType
+
+B, S, D = 2, 2048, 128
+P = 128
+PACK = 4
+K_PASS = P * PACK
+PASSES = S // K_PASS
+Q_TILES = S // P
+BANK = 512
+STORE_TILES = 4
+MASKED = 1.0e30
+
+FLOPS = 2 * 2 * B * S * S * D
+
+
+def prepare_batch(nc, pools, ident_bf, b, q_scaled, k, v, mask):
+    keep, stage, psum_tr = pools["keep"], pools["stage"], pools["psum_tr"]
+
+    q_sb = keep.tile([P, Q_TILES, D], BF16, name="q_sb%d" % b)
+    nc.sync.dma_start(out=q_sb[:], in_=q_scaled[b].rearrange("(p t) d -> p t d", t=Q_TILES))
+    k_sb = stage.tile([P, PASSES, PACK, D], BF16, name="k_sb")
+    nc.sync.dma_start(out=k_sb[:], in_=k[b].rearrange("(g p t) d -> p g t d", g=PASSES, t=PACK))
+    v_sb = stage.tile([P, PASSES, PACK, D], BF16, name="v_sb")
+    nc.sync.dma_start(out=v_sb[:], in_=v[b].rearrange("(g p t) d -> p g t d", g=PASSES, t=PACK))
+    mask_all = stage.tile([P, S], BF16, name="mask_all")
+    nc.scalar.dma_start(out=mask_all[:], in_=mask[b].partition_broadcast(P))
+    mask_q = stage.tile([P, Q_TILES], BF16, name="mask_q")
+    nc.scalar.dma_start(out=mask_q[:], in_=mask[b].rearrange("(p t) -> p t", t=Q_TILES))
+
+    qT = keep.tile([P, Q_TILES, P], BF16, name="qT%d" % b)
+    for half in range(2):
+        q_tr = psum_tr.tile([P, 8, P], BF16, tag="tr", name="q_tr")
+        for j in range(8):
+            nc.tensor.transpose(q_tr[:, j, :], q_sb[:, 8 * half + j, :], ident_bf[:])
+        nc.scalar.copy(out=qT[:, 8 * half : 8 * half + 8, :], in_=q_tr[:])
+
+    kT = keep.tile([P, PASSES, K_PASS], BF16, name="kT%d" % b)
+    for g in range(PASSES):
+        k_tr = psum_tr.tile([P, PACK, P], BF16, tag="tr", name="k_tr")
+        for t in range(PACK):
+            nc.tensor.transpose(k_tr[:, t, :], k_sb[:, g, t, :], ident_bf[:])
+        nc.vector.tensor_copy(
+            out=kT[:, g, :].rearrange("d (u p e) -> d u p e", u=2, e=2),
+            in_=k_tr[:].rearrange("d (u e) p -> d u p e", e=2),
+        )
+
+    log_mask = keep.tile([P, PASSES, K_PASS], BF16, name="log_mask%d" % b)
+    for g in range(PASSES):
+        nc.gpsimd.tensor_scalar(
+            out=log_mask[:, g, :].rearrange("q (u p e) -> q u p e", u=2, e=2),
+            in0=mask_all[:, g * K_PASS : (g + 1) * K_PASS].rearrange("q (p u e) -> q u p e", u=2, e=2),
+            scalar1=-1.0,
+            scalar2=MASKED,
+            op0=ALU.add,
+            op1=ALU.mult,
+        )
+
+    v_grouped = stage.tile([P, PASSES, D, PACK], BF16, name="v_grouped", align_bytes=64)
+    nc.vector.tensor_copy(out=v_grouped[:], in_=v_sb[:].rearrange("p g t d -> p g d t"))
+    v_codes = keep.tile([P, PASSES * D], U32, name="v_codes%d" % b, align_bytes=64)
+    v_scales = keep.tile([P, PASSES * D], U8, name="v_scales%d" % b, align_bytes=64)
+    nc.vector.quantize_mx(
+        out=v_codes[:].bitcast(FP8X4),
+        scales=v_scales[:],
+        in_=v_grouped[:].rearrange("p g d t -> p (g d t)"),
+    )
+
+    keep_q = keep.tile([P, Q_TILES], F32, name="keep_q%d" % b)
+    nc.gpsimd.tensor_copy(out=keep_q[:], in_=mask_q[:])
+    drop_q = stage.tile([P, Q_TILES], F32, name="drop_q")
+    nc.gpsimd.tensor_scalar(
+        out=drop_q[:], in0=mask_q[:], scalar1=-1.0, scalar2=1.0, op0=ALU.mult, op1=ALU.add
+    )
+    q_dropped = keep.tile([P, Q_TILES, D], BF16, name="q_dropped%d" % b)
+    nc.gpsimd.tensor_tensor(
+        out=q_dropped[:],
+        in0=q_sb[:],
+        in1=drop_q[:].unsqueeze(2).to_broadcast([P, Q_TILES, D]),
+        op=ALU.mult,
+    )
+    return {
+        "qT": qT,
+        "kT": kT,
+        "log_mask": log_mask,
+        "v_codes": v_codes,
+        "v_scales": v_scales,
+        "keep_q": keep_q,
+        "q_dropped": q_dropped,
+    }
+
+
+def attend_query_tile(nc, pools, ident_f32, ops, t, out_rows):
+    work, small = pools["work"], pools["small"]
+    psum_s, psum_tr, psum_acc = pools["psum_s"], pools["psum_tr"], pools["psum_acc"]
+
+    scores = work.tile([P, PASSES, K_PASS], F32, name="scores")
+    for g in range(PASSES):
+        s_ps = psum_s.tile([P, BANK], F32, name="s_ps")
+        nc.tensor.matmul(out=s_ps[:], lhsT=ops["qT"][:, t, :], rhs=ops["kT"][:, g, :], start=True, stop=True)
+        nc.vector.tensor_tensor(out=scores[:, g, :], in0=s_ps[:], in1=ops["log_mask"][:, g, :], op=ALU.add)
+
+    neg_max = small.tile([P, 1], F32, name="neg_max")
+    nc.vector.tensor_reduce(
+        out=neg_max[:], in_=scores[:].rearrange("p g c -> p (g c)"), axis=AX.X, op=ALU.max, negate=True
+    )
+    e_sb = work.tile([P, S], BF16, name="e_sb")
+    row_sum = small.tile([P, 1], F32, name="row_sum")
+    nc.scalar.activation(
+        out=e_sb[:],
+        in_=scores[:].rearrange("p g c -> p (g c)"),
+        func=ACT.Exp,
+        bias=neg_max[:],
+        scale=1.0,
+        accum_out=row_sum[:],
+    )
+
+    e_words = e_sb[:].bitcast(F32)
+    grouped = work.tile([P, S], BF16, name="grouped", align_bytes=64)
+    grouped_words = grouped[:].bitcast(F32).rearrange("p (g i u) -> p g i u", g=PASSES, u=2)
+    for half in range(2):
+        e_tr = psum_tr.tile([P, 2, 2, P], F32, tag="tr", name="e_tr")
+        for gg in range(2):
+            for u in range(2):
+                first = ((2 * half + gg) * 2 + u) * P
+                nc.tensor.transpose(e_tr[:, gg, u, :], e_words[:, first : first + P], ident_f32[:])
+        nc.scalar.copy(
+            out=grouped_words[:, 2 * half : 2 * half + 2, :, :],
+            in_=e_tr[:].rearrange("p g u i -> p g i u"),
+        )
+
+    e_codes = work.tile([P, PASSES * P], U32, name="e_codes", align_bytes=64)
+    e_scales = work.tile([P, PASSES * P], U8, name="e_scales", align_bytes=64)
+    nc.vector.quantize_mx(out=e_codes[:].bitcast(FP8X4), scales=e_scales[:], in_=grouped[:])
+
+    acc = psum_acc.tile([P, D], F32, name="acc")
+    for g in range(PASSES):
+        cols = slice(g * P, (g + 1) * P)
+        nc.tensor.matmul_mx(
+            out=acc[:],
+            lhsT=e_codes[:, cols].bitcast(FP8X4),
+            lhsT_scale=e_scales[:, cols],
+            rhs=ops["v_codes"][:, cols].bitcast(FP8X4),
+            rhs_scale=ops["v_scales"][:, cols],
+            start=(g == 0),
+            stop=(g == PASSES - 1),
+        )
+
+    weight = small.tile([P, 1], F32, name="weight")
+    nc.vector.reciprocal(out=weight[:], in_=row_sum[:])
+    weight_kept = small.tile([P, 1], F32, name="weight_kept")
+    nc.vector.tensor_tensor(out=weight_kept[:], in0=weight[:], in1=ops["keep_q"][:, t : t + 1], op=ALU.mult)
+    nc.vector.scalar_tensor_tensor(
+        out=out_rows,
+        in0=acc[:],
+        scalar=weight_kept[:],
+        in1=ops["q_dropped"][:, t, :],
+        op0=ALU.mult,
+        op1=ALU.add,
+    )
+
+
+def tile_attention_pa_kernel(tc, q_scaled, k, v, mask, out):
+    nc = tc.nc
+    with ExitStack() as ctx:
+        pools = {
+            "keep": ctx.enter_context(tc.tile_pool(name="keep", bufs=1)),
+            "stage": ctx.enter_context(tc.tile_pool(name="stage", bufs=2)),
+            "work": ctx.enter_context(tc.tile_pool(name="work", bufs=3)),
+            "small": ctx.enter_context(tc.tile_pool(name="small", bufs=4)),
+            "psum_s": ctx.enter_context(tc.psum_pool(name="psum_s", bufs=4)),
+            "psum_tr": ctx.enter_context(tc.psum_pool(name="psum_tr", bufs=2)),
+            "psum_acc": ctx.enter_context(tc.psum_pool(name="psum_acc", bufs=2)),
+        }
+        ident_bf = pools["keep"].tile([P, P], BF16, name="ident_bf")
+        make_identity(nc, ident_bf[:])
+        ident_f32 = pools["keep"].tile([P, P], F32, name="ident_f32")
+        make_identity(nc, ident_f32[:])
+
+        batches = [prepare_batch(nc, pools, ident_bf, b, q_scaled, k, v, mask) for b in range(B)]
+
+        for b in range(B):
+            out_view = out[b].rearrange("(p t) d -> p t d", t=Q_TILES)
+            for first in range(0, Q_TILES, STORE_TILES):
+                out_sb = pools["work"].tile([P, STORE_TILES, D], F32, name="out_sb")
+                for j in range(STORE_TILES):
+                    attend_query_tile(nc, pools, ident_f32, batches[b], first + j, out_sb[:, j, :])
+                nc.sync.dma_start(out=out_view[:, first : first + STORE_TILES, :], in_=out_sb[:])

@@ -67,6 +67,16 @@ def prepare_batch(nc, pools, ident_bf, b, q_scaled, k, v, mask):
             op1=ALU.mult,
         )
 
+    log_mask_col = keep.tile([P, S // P], F32, name="log_mask_col%d" % b)
+    for half in range(2):
+        m_tr = psum_tr.tile([P, 8, P], BF16, tag="tr", name="m_tr")
+        for j in range(8):
+            first = (8 * half + j) * P
+            nc.tensor.transpose(
+                m_tr[:, j, :], log_mask[:].rearrange("q g c -> q (g c)")[:, first : first + P], ident_bf[:]
+            )
+        nc.vector.tensor_copy(out=log_mask_col[:, 8 * half : 8 * half + 8], in_=m_tr[:, :, 0])
+
     v_grouped = stage.tile([P, PASSES, D, PACK], BF16, name="v_grouped", align_bytes=64)
     nc.vector.tensor_copy(out=v_grouped[:], in_=v_sb[:].rearrange("p g t d -> p g d t"))
     v_codes = keep.tile([P, PASSES * D], U32, name="v_codes%d" % b, align_bytes=64)
@@ -93,7 +103,7 @@ def prepare_batch(nc, pools, ident_bf, b, q_scaled, k, v, mask):
     return {
         "qT": qT,
         "kT": kT,
-        "log_mask": log_mask,
+        "log_mask_col": log_mask_col,
         "v_codes": v_codes,
         "v_scales": v_scales,
         "keep_q": keep_q,
@@ -101,32 +111,48 @@ def prepare_batch(nc, pools, ident_bf, b, q_scaled, k, v, mask):
     }
 
 
-def attend_query_tile(nc, pools, ident_f32, ops, t, out_rows):
+def attend_query_tile(nc, pools, ident_f32, ops, t, acc, row_sum):
     work, small = pools["work"], pools["small"]
-    psum_s, psum_tr, psum_acc = pools["psum_s"], pools["psum_tr"], pools["psum_acc"]
+    psum_s, psum_tr = pools["psum_s"], pools["psum_tr"]
 
-    scores = work.tile([P, PASSES, K_PASS], F32, name="scores")
+    neg_scores = work.tile([P, PASSES, K_PASS], F32, name="neg_scores")
+    part_min = small.tile([P, PASSES], F32, name="part_min")
     for g in range(PASSES):
         s_ps = psum_s.tile([P, BANK], F32, name="s_ps")
-        nc.tensor.matmul(out=s_ps[:], lhsT=ops["qT"][:, t, :], rhs=ops["kT"][:, g, :], start=True, stop=True)
-        nc.vector.tensor_tensor(out=scores[:, g, :], in0=s_ps[:], in1=ops["log_mask"][:, g, :], op=ALU.add)
+        for r in range(BANK // P):
+            j = g * (BANK // P) + r
+            nc.tensor.matmul(
+                out=s_ps[:, r * P : (r + 1) * P],
+                lhsT=ops["log_mask_col"][:, j : j + 1].to_broadcast([P, P]),
+                rhs=ident_f32[:],
+                is_transpose=True,
+                start=(r == 0),
+                stop=False,
+            )
+        nc.tensor.matmul(out=s_ps[:], lhsT=ops["qT"][:, t, :], rhs=ops["kT"][:, g, :], start=False, stop=True)
+        nc.vector.tensor_scalar(
+            out=neg_scores[:, g, :],
+            in0=s_ps[:],
+            scalar1=-1.0,
+            scalar2=None,
+            op0=ALU.mult,
+            op1=ALU.min,
+            accum_out=part_min[:, g : g + 1],
+        )
 
     neg_max = small.tile([P, 1], F32, name="neg_max")
-    nc.vector.tensor_reduce(
-        out=neg_max[:], in_=scores[:].rearrange("p g c -> p (g c)"), axis=AX.X, op=ALU.max, negate=True
-    )
-    e_sb = work.tile([P, S], BF16, name="e_sb")
-    row_sum = small.tile([P, 1], F32, name="row_sum")
+    nc.vector.tensor_reduce(out=neg_max[:], in_=part_min[:], axis=AX.X, op=ALU.min)
+    e_sb = work.tile([P, PASSES, K_PASS], BF16, name="e_sb")
     nc.scalar.activation(
-        out=e_sb[:],
-        in_=scores[:].rearrange("p g c -> p (g c)"),
+        out=e_sb[:].rearrange("p g c -> p (g c)"),
+        in_=neg_scores[:].rearrange("p g c -> p (g c)"),
         func=ACT.Exp,
         bias=neg_max[:],
-        scale=1.0,
-        accum_out=row_sum[:],
+        scale=-1.0,
+        accum_out=row_sum,
     )
 
-    e_words = e_sb[:].bitcast(F32)
+    e_words = e_sb[:].rearrange("p g c -> p (g c)").bitcast(F32)
     grouped = work.tile([P, S], BF16, name="grouped", align_bytes=64)
     grouped_words = grouped[:].bitcast(F32).rearrange("p (g i u) -> p g i u", g=PASSES, u=2)
     for half in range(2):
@@ -144,11 +170,10 @@ def attend_query_tile(nc, pools, ident_f32, ops, t, out_rows):
     e_scales = work.tile([P, PASSES * P], U8, name="e_scales", align_bytes=64)
     nc.vector.quantize_mx(out=e_codes[:].bitcast(FP8X4), scales=e_scales[:], in_=grouped[:])
 
-    acc = psum_acc.tile([P, D], F32, name="acc")
     for g in range(PASSES):
         cols = slice(g * P, (g + 1) * P)
         nc.tensor.matmul_mx(
-            out=acc[:],
+            out=acc,
             lhsT=e_codes[:, cols].bitcast(FP8X4),
             lhsT_scale=e_scales[:, cols],
             rhs=ops["v_codes"][:, cols].bitcast(FP8X4),
@@ -156,19 +181,6 @@ def attend_query_tile(nc, pools, ident_f32, ops, t, out_rows):
             start=(g == 0),
             stop=(g == PASSES - 1),
         )
-
-    weight = small.tile([P, 1], F32, name="weight")
-    nc.vector.reciprocal(out=weight[:], in_=row_sum[:])
-    weight_kept = small.tile([P, 1], F32, name="weight_kept")
-    nc.vector.tensor_tensor(out=weight_kept[:], in0=weight[:], in1=ops["keep_q"][:, t : t + 1], op=ALU.mult)
-    nc.vector.scalar_tensor_tensor(
-        out=out_rows,
-        in0=acc[:],
-        scalar=weight_kept[:],
-        in1=ops["q_dropped"][:, t, :],
-        op0=ALU.mult,
-        op1=ALU.add,
-    )
 
 
 def tile_attention_pa_kernel(tc, q_scaled, k, v, mask, out):
@@ -193,7 +205,22 @@ def tile_attention_pa_kernel(tc, q_scaled, k, v, mask, out):
         for b in range(B):
             out_view = out[b].rearrange("(p t) d -> p t d", t=Q_TILES)
             for first in range(0, Q_TILES, STORE_TILES):
+                tiles = slice(first, first + STORE_TILES)
+                acc = pools["psum_acc"].tile([P, STORE_TILES, D], F32, name="acc")
+                row_sums = pools["small"].tile([P, STORE_TILES], F32, name="row_sums")
+                for j in range(STORE_TILES):
+                    attend_query_tile(nc, pools, ident_f32, batches[b], first + j, acc[:, j, :], row_sums[:, j : j + 1])
+                weight = pools["small"].tile([P, STORE_TILES], F32, name="weight")
+                nc.vector.reciprocal(out=weight[:], in_=row_sums[:])
+                nc.vector.tensor_tensor(out=weight[:], in0=weight[:], in1=batches[b]["keep_q"][:, tiles], op=ALU.mult)
                 out_sb = pools["work"].tile([P, STORE_TILES, D], F32, name="out_sb")
                 for j in range(STORE_TILES):
-                    attend_query_tile(nc, pools, ident_f32, batches[b], first + j, out_sb[:, j, :])
-                nc.sync.dma_start(out=out_view[:, first : first + STORE_TILES, :], in_=out_sb[:])
+                    nc.vector.scalar_tensor_tensor(
+                        out=out_sb[:, j, :],
+                        in0=acc[:, j, :],
+                        scalar=weight[:, j : j + 1],
+                        in1=batches[b]["q_dropped"][:, first + j, :],
+                        op0=ALU.mult,
+                        op1=ALU.add,
+                    )
+                nc.sync.dma_start(out=out_view[:, tiles, :], in_=out_sb[:])

@@ -19,32 +19,54 @@ K_PASS = P * PACK
 PASSES = S // K_PASS
 Q_TILES = S // P
 BANK = 512
+BLOCKS = BANK // P
 STORE_TILES = 4
 MASKED = 1.0e30
+AHEAD = 2
+PREPARE_NEXT_AT = 4
 
 FLOPS = 2 * 2 * B * S * S * D
 
 
-def prepare_batch(nc, pools, ident_bf, b, q_scaled, k, v, mask):
-    keep, stage, psum_tr = pools["keep"], pools["stage"], pools["psum_tr"]
-
+def load_batch(nc, pools, b, q_scaled, k, v, mask):
+    keep = pools["keep"]
+    mask_rows = keep.tile([P, P], BF16, name="mask_rows%d" % b)
+    nc.gpsimd.memset(mask_rows[:], 0.0)
+    by_column = mask[b].rearrange("(ga h u e) -> u ga h e", ga=2 * PASSES, u=2, e=2)
+    for u in range(2):
+        rows = slice(2 * PASSES * u, 2 * PASSES * (u + 1))
+        nc.scalar.dma_start(out=mask_rows[rows, :].rearrange("r (h e) -> r h e", e=2), in_=by_column[u])
+    mask_q = keep.tile([P, Q_TILES], BF16, name="mask_q%d" % b)
+    nc.scalar.dma_start(out=mask_q[:], in_=mask[b].rearrange("(p t) -> p t", t=Q_TILES))
+    k_sb = keep.tile([P, PASSES, PACK, D], BF16, name="k_sb%d" % b)
+    nc.sync.dma_start(out=k_sb[:], in_=k[b].rearrange("(g p t) d -> p g t d", g=PASSES, t=PACK))
     q_sb = keep.tile([P, Q_TILES, D], BF16, name="q_sb%d" % b)
     nc.sync.dma_start(out=q_sb[:], in_=q_scaled[b].rearrange("(p t) d -> p t d", t=Q_TILES))
-    k_sb = stage.tile([P, PASSES, PACK, D], BF16, name="k_sb")
-    nc.sync.dma_start(out=k_sb[:], in_=k[b].rearrange("(g p t) d -> p g t d", g=PASSES, t=PACK))
-    v_sb = stage.tile([P, PASSES, PACK, D], BF16, name="v_sb")
+    v_sb = keep.tile([P, PASSES, PACK, D], BF16, name="v_sb%d" % b)
     nc.sync.dma_start(out=v_sb[:], in_=v[b].rearrange("(g p t) d -> p g t d", g=PASSES, t=PACK))
-    mask_all = stage.tile([P, S], BF16, name="mask_all")
-    nc.scalar.dma_start(out=mask_all[:], in_=mask[b].partition_broadcast(P))
-    mask_q = stage.tile([P, Q_TILES], BF16, name="mask_q")
-    nc.scalar.dma_start(out=mask_q[:], in_=mask[b].rearrange("(p t) -> p t", t=Q_TILES))
+    return {"b": b, "mask_rows": mask_rows, "mask_q": mask_q, "k_sb": k_sb, "q_sb": q_sb, "v_sb": v_sb}
 
-    qT = keep.tile([P, Q_TILES, P], BF16, name="qT%d" % b)
-    for half in range(2):
-        q_tr = psum_tr.tile([P, 8, P], BF16, tag="tr", name="q_tr")
-        for j in range(8):
-            nc.tensor.transpose(q_tr[:, j, :], q_sb[:, 8 * half + j, :], ident_bf[:])
-        nc.scalar.copy(out=qT[:, 8 * half : 8 * half + 8, :], in_=q_tr[:])
+
+def prepare_batch(nc, pools, ident_bf, loaded):
+    keep, psum_tr = pools["keep"], pools["psum_tr"]
+    b, q_sb, k_sb, v_sb = loaded["b"], loaded["q_sb"], loaded["k_sb"], loaded["v_sb"]
+
+    m_tr = psum_tr.tile([P, P], BF16, tag="tr", name="m_tr")
+    nc.tensor.transpose(m_tr[:], loaded["mask_rows"][:], ident_bf[:])
+    mask_col = keep.tile([P, S // P], F32, name="mask_col%d" % b)
+    nc.vector.tensor_copy(
+        out=mask_col[:].rearrange("n (g u a) -> n g u a", u=2, a=2),
+        in_=m_tr[:, 0 : S // P].rearrange("n (u g a) -> n g u a", u=2, a=2),
+    )
+    log_mask = keep.tile([P, S // P, P], F32, name="log_mask%d" % b)
+    nc.gpsimd.tensor_scalar(
+        out=log_mask[:],
+        in0=mask_col[:].unsqueeze(2).to_broadcast([P, S // P, P]),
+        scalar1=-1.0,
+        scalar2=MASKED,
+        op0=ALU.add,
+        op1=ALU.mult,
+    )
 
     kT = keep.tile([P, PASSES, K_PASS], BF16, name="kT%d" % b)
     for g in range(PASSES):
@@ -56,28 +78,14 @@ def prepare_batch(nc, pools, ident_bf, b, q_scaled, k, v, mask):
             in_=k_tr[:].rearrange("d (u e) p -> d u p e", e=2),
         )
 
-    log_mask = keep.tile([P, PASSES, K_PASS], BF16, name="log_mask%d" % b)
-    for g in range(PASSES):
-        nc.gpsimd.tensor_scalar(
-            out=log_mask[:, g, :].rearrange("q (u p e) -> q u p e", u=2, e=2),
-            in0=mask_all[:, g * K_PASS : (g + 1) * K_PASS].rearrange("q (p u e) -> q u p e", u=2, e=2),
-            scalar1=-1.0,
-            scalar2=MASKED,
-            op0=ALU.add,
-            op1=ALU.mult,
-        )
-
-    log_mask_col = keep.tile([P, S // P], F32, name="log_mask_col%d" % b)
+    qT = keep.tile([P, Q_TILES, P], BF16, name="qT%d" % b)
     for half in range(2):
-        m_tr = psum_tr.tile([P, 8, P], BF16, tag="tr", name="m_tr")
-        for j in range(8):
-            first = (8 * half + j) * P
-            nc.tensor.transpose(
-                m_tr[:, j, :], log_mask[:].rearrange("q g c -> q (g c)")[:, first : first + P], ident_bf[:]
-            )
-        nc.vector.tensor_copy(out=log_mask_col[:, 8 * half : 8 * half + 8], in_=m_tr[:, :, 0])
+        q_tr = psum_tr.tile([P, Q_TILES // 2, P], BF16, tag="tr", name="q_tr")
+        for j in range(Q_TILES // 2):
+            nc.tensor.transpose(q_tr[:, j, :], q_sb[:, (Q_TILES // 2) * half + j, :], ident_bf[:])
+        nc.scalar.copy(out=qT[:, (Q_TILES // 2) * half : (Q_TILES // 2) * (half + 1), :], in_=q_tr[:])
 
-    v_grouped = stage.tile([P, PASSES, D, PACK], BF16, name="v_grouped", align_bytes=64)
+    v_grouped = keep.tile([P, PASSES, D, PACK], BF16, name="v_grouped%d" % b, align_bytes=64)
     nc.vector.tensor_copy(out=v_grouped[:], in_=v_sb[:].rearrange("p g t d -> p g d t"))
     v_codes = keep.tile([P, PASSES * D], U32, name="v_codes%d" % b, align_bytes=64)
     v_scales = keep.tile([P, PASSES * D], U8, name="v_scales%d" % b, align_bytes=64)
@@ -88,10 +96,10 @@ def prepare_batch(nc, pools, ident_bf, b, q_scaled, k, v, mask):
     )
 
     keep_q = keep.tile([P, Q_TILES], F32, name="keep_q%d" % b)
-    nc.gpsimd.tensor_copy(out=keep_q[:], in_=mask_q[:])
-    drop_q = stage.tile([P, Q_TILES], F32, name="drop_q")
+    nc.gpsimd.tensor_copy(out=keep_q[:], in_=loaded["mask_q"][:])
+    drop_q = keep.tile([P, Q_TILES], F32, name="drop_q%d" % b)
     nc.gpsimd.tensor_scalar(
-        out=drop_q[:], in0=mask_q[:], scalar1=-1.0, scalar2=1.0, op0=ALU.mult, op1=ALU.add
+        out=drop_q[:], in0=loaded["mask_q"][:], scalar1=-1.0, scalar2=1.0, op0=ALU.mult, op1=ALU.add
     )
     q_dropped = keep.tile([P, Q_TILES, D], BF16, name="q_dropped%d" % b)
     nc.gpsimd.tensor_tensor(
@@ -103,7 +111,7 @@ def prepare_batch(nc, pools, ident_bf, b, q_scaled, k, v, mask):
     return {
         "qT": qT,
         "kT": kT,
-        "log_mask_col": log_mask_col,
+        "log_mask": log_mask,
         "v_codes": v_codes,
         "v_scales": v_scales,
         "keep_q": keep_q,
@@ -111,65 +119,63 @@ def prepare_batch(nc, pools, ident_bf, b, q_scaled, k, v, mask):
     }
 
 
-def attend_query_tile(nc, pools, ident_f32, ops, t, acc, row_sum):
-    work, small = pools["work"], pools["small"]
-    psum_s, psum_tr = pools["psum_s"], pools["psum_tr"]
-
-    neg_scores = work.tile([P, PASSES, K_PASS], F32, name="neg_scores")
-    part_min = small.tile([P, PASSES], F32, name="part_min")
-    for g in range(PASSES):
-        s_ps = psum_s.tile([P, BANK], F32, name="s_ps")
-        for r in range(BANK // P):
-            j = g * (BANK // P) + r
-            nc.tensor.matmul(
-                out=s_ps[:, r * P : (r + 1) * P],
-                lhsT=ops["log_mask_col"][:, j : j + 1].to_broadcast([P, P]),
-                rhs=ident_f32[:],
-                is_transpose=True,
-                start=(r == 0),
-                stop=False,
-            )
-        nc.tensor.matmul(out=s_ps[:], lhsT=ops["qT"][:, t, :], rhs=ops["kT"][:, g, :], start=False, stop=True)
-        nc.vector.tensor_scalar(
-            out=neg_scores[:, g, :],
-            in0=s_ps[:],
-            scalar1=-1.0,
-            scalar2=None,
-            op0=ALU.mult,
-            op1=ALU.min,
-            accum_out=part_min[:, g : g + 1],
+def score_bank(nc, pools, ident_f32, ops, t, g, neg_scores, part_min):
+    s_ps = pools["psum_s"].tile([P, BANK], F32, name="s_ps")
+    for r in range(BLOCKS):
+        nc.tensor.matmul(
+            out=s_ps[:, r * P : (r + 1) * P],
+            lhsT=ops["log_mask"][:, g * BLOCKS + r, :],
+            rhs=ident_f32[:],
+            is_transpose=True,
+            start=(r == 0),
+            stop=False,
         )
+    nc.tensor.matmul(out=s_ps[:], lhsT=ops["qT"][:, t, :], rhs=ops["kT"][:, g, :], start=False, stop=True)
+    nc.vector.tensor_scalar(
+        out=neg_scores[:, g, :],
+        in0=s_ps[:],
+        scalar1=-1.0,
+        scalar2=None,
+        op0=ALU.mult,
+        op1=ALU.min,
+        accum_out=part_min[:, g : g + 1],
+    )
 
-    neg_max = small.tile([P, 1], F32, name="neg_max")
-    nc.vector.tensor_reduce(out=neg_max[:], in_=part_min[:], axis=AX.X, op=ALU.min)
-    e_sb = work.tile([P, PASSES, K_PASS], BF16, name="e_sb")
+
+def exponentials(nc, pools, neg_scores, neg_max, row_sum):
+    e_sb = pools["work"].tile([P, S], BF16, name="e_sb")
     nc.scalar.activation(
-        out=e_sb[:].rearrange("p g c -> p (g c)"),
+        out=e_sb[:],
         in_=neg_scores[:].rearrange("p g c -> p (g c)"),
         func=ACT.Exp,
         bias=neg_max[:],
         scale=-1.0,
         accum_out=row_sum,
     )
+    return e_sb
 
-    e_words = e_sb[:].rearrange("p g c -> p (g c)").bitcast(F32)
-    grouped = work.tile([P, S], BF16, name="grouped", align_bytes=64)
+
+def transpose_half(nc, pools, ident_f32, e_sb, half):
+    e_words = e_sb[:].bitcast(F32)
+    e_tr = pools["psum_tr"].tile([P, 2, 2, P], F32, tag="tr", name="e_tr")
+    for gg in range(2):
+        for u in range(2):
+            first = ((2 * half + gg) * 2 + u) * P
+            nc.tensor.transpose(e_tr[:, gg, u, :], e_words[:, first : first + P], ident_f32[:])
+    return e_tr
+
+
+def copy_half(nc, e_tr, grouped, half):
     grouped_words = grouped[:].bitcast(F32).rearrange("p (g i u) -> p g i u", g=PASSES, u=2)
-    for half in range(2):
-        e_tr = psum_tr.tile([P, 2, 2, P], F32, tag="tr", name="e_tr")
-        for gg in range(2):
-            for u in range(2):
-                first = ((2 * half + gg) * 2 + u) * P
-                nc.tensor.transpose(e_tr[:, gg, u, :], e_words[:, first : first + P], ident_f32[:])
-        nc.scalar.copy(
-            out=grouped_words[:, 2 * half : 2 * half + 2, :, :],
-            in_=e_tr[:].rearrange("p g u i -> p g i u"),
-        )
+    nc.scalar.copy(
+        out=grouped_words[:, 2 * half : 2 * half + 2, :, :], in_=e_tr[:].rearrange("p g u i -> p g i u")
+    )
 
-    e_codes = work.tile([P, PASSES * P], U32, name="e_codes", align_bytes=64)
-    e_scales = work.tile([P, PASSES * P], U8, name="e_scales", align_bytes=64)
+
+def quantise_and_multiply(nc, pools, ops, grouped, acc):
+    e_codes = pools["work"].tile([P, PASSES * P], U32, name="e_codes", align_bytes=64)
+    e_scales = pools["work"].tile([P, PASSES * P], U8, name="e_scales", align_bytes=64)
     nc.vector.quantize_mx(out=e_codes[:].bitcast(FP8X4), scales=e_scales[:], in_=grouped[:])
-
     for g in range(PASSES):
         cols = slice(g * P, (g + 1) * P)
         nc.tensor.matmul_mx(
@@ -183,44 +189,95 @@ def attend_query_tile(nc, pools, ident_f32, ops, t, acc, row_sum):
         )
 
 
+def finish_tiles(nc, pools, ops, first, acc, row_sums, out_rows):
+    tiles = slice(first, first + STORE_TILES)
+    weight = pools["small"].tile([P, STORE_TILES], F32, name="weight")
+    nc.vector.reciprocal(out=weight[:], in_=row_sums[:])
+    weight_kept = pools["small"].tile([P, STORE_TILES], F32, name="weight_kept")
+    nc.vector.tensor_tensor(out=weight_kept[:], in0=weight[:], in1=ops["keep_q"][:, tiles], op=ALU.mult)
+    out_sb = pools["work"].tile([P, STORE_TILES, D], F32, name="out_sb")
+    for j in range(STORE_TILES):
+        nc.vector.scalar_tensor_tensor(
+            out=out_sb[:, j, :],
+            in0=acc[:, j, :],
+            scalar=weight_kept[:, j : j + 1],
+            in1=ops["q_dropped"][:, first + j, :],
+            op0=ALU.mult,
+            op1=ALU.add,
+        )
+    nc.sync.dma_start(out=out_rows[:, tiles, :], in_=out_sb[:])
+
+
 def tile_attention_pa_kernel(tc, q_scaled, k, v, mask, out):
     nc = tc.nc
     with ExitStack() as ctx:
         pools = {
             "keep": ctx.enter_context(tc.tile_pool(name="keep", bufs=1)),
-            "stage": ctx.enter_context(tc.tile_pool(name="stage", bufs=2)),
-            "work": ctx.enter_context(tc.tile_pool(name="work", bufs=3)),
-            "small": ctx.enter_context(tc.tile_pool(name="small", bufs=4)),
+            "scores": ctx.enter_context(tc.tile_pool(name="scores", bufs=AHEAD + 1)),
+            "work": ctx.enter_context(tc.tile_pool(name="work", bufs=2)),
+            "small": ctx.enter_context(tc.tile_pool(name="small", bufs=AHEAD + 2)),
             "psum_s": ctx.enter_context(tc.psum_pool(name="psum_s", bufs=4)),
-            "psum_tr": ctx.enter_context(tc.psum_pool(name="psum_tr", bufs=2)),
-            "psum_acc": ctx.enter_context(tc.psum_pool(name="psum_acc", bufs=2)),
+            "psum_tr": ctx.enter_context(tc.psum_pool(name="psum_tr", bufs=3)),
+            "psum_acc": ctx.enter_context(tc.psum_pool(name="psum_acc", bufs=1)),
         }
         ident_bf = pools["keep"].tile([P, P], BF16, name="ident_bf")
         make_identity(nc, ident_bf[:])
         ident_f32 = pools["keep"].tile([P, P], F32, name="ident_f32")
         make_identity(nc, ident_f32[:])
 
-        batches = [prepare_batch(nc, pools, ident_bf, b, q_scaled, k, v, mask) for b in range(B)]
+        loaded = [load_batch(nc, pools, b, q_scaled, k, v, mask) for b in range(B)]
+        batches = {0: prepare_batch(nc, pools, ident_bf, loaded[0])}
+        out_rows = [out[b].rearrange("(p t) d -> p t d", t=Q_TILES) for b in range(B)]
 
-        for b in range(B):
-            out_view = out[b].rearrange("(p t) d -> p t d", t=Q_TILES)
-            for first in range(0, Q_TILES, STORE_TILES):
-                tiles = slice(first, first + STORE_TILES)
-                acc = pools["psum_acc"].tile([P, STORE_TILES, D], F32, name="acc")
-                row_sums = pools["small"].tile([P, STORE_TILES], F32, name="row_sums")
-                for j in range(STORE_TILES):
-                    attend_query_tile(nc, pools, ident_f32, batches[b], first + j, acc[:, j, :], row_sums[:, j : j + 1])
-                weight = pools["small"].tile([P, STORE_TILES], F32, name="weight")
-                nc.vector.reciprocal(out=weight[:], in_=row_sums[:])
-                nc.vector.tensor_tensor(out=weight[:], in0=weight[:], in1=batches[b]["keep_q"][:, tiles], op=ALU.mult)
-                out_sb = pools["work"].tile([P, STORE_TILES, D], F32, name="out_sb")
-                for j in range(STORE_TILES):
-                    nc.vector.scalar_tensor_tensor(
-                        out=out_sb[:, j, :],
-                        in0=acc[:, j, :],
-                        scalar=weight[:, j : j + 1],
-                        in1=batches[b]["q_dropped"][:, first + j, :],
-                        op0=ALU.mult,
-                        op1=ALU.add,
-                    )
-                nc.sync.dma_start(out=out_view[:, tiles, :], in_=out_sb[:])
+        n_tiles = B * Q_TILES
+        neg_scores, part_min, neg_max, e_tr, grouped, row_sums, acc = {}, {}, {}, {}, {}, {}, {}
+
+        def scores(n, banks):
+            if n >= n_tiles:
+                return
+            if 0 in banks:
+                neg_scores[n] = pools["scores"].tile([P, PASSES, K_PASS], F32, name="neg_scores")
+                part_min[n] = pools["small"].tile([P, PASSES], F32, name="part_min")
+            for g in banks:
+                score_bank(nc, pools, ident_f32, batches[n // Q_TILES], n % Q_TILES, g, neg_scores[n], part_min[n])
+            if PASSES - 1 in banks:
+                neg_max[n] = pools["small"].tile([P, 1], F32, name="neg_max")
+                nc.vector.tensor_reduce(out=neg_max[n][:], in_=part_min[n][:], axis=AX.X, op=ALU.min)
+
+        with tc.manual_schedule():
+            for n in range(AHEAD):
+                scores(n, range(PASSES))
+            for n in range(n_tiles + 2):
+                group = n // STORE_TILES
+                if n < n_tiles:
+                    if n % STORE_TILES == 0:
+                        row_sums[group] = pools["small"].tile([P, STORE_TILES], F32, name="row_sums")
+                    j = n % STORE_TILES
+                    e_sb = exponentials(nc, pools, neg_scores[n], neg_max[n], row_sums[group][:, j : j + 1])
+                scores(n + AHEAD, range(1))
+                done = n - 2
+                if done >= 0:
+                    done_group, j = done // STORE_TILES, done % STORE_TILES
+                    ops = batches[done // Q_TILES]
+                    if j == 0:
+                        acc[done_group] = pools["psum_acc"].tile([P, STORE_TILES, D], F32, name="acc")
+                    quantise_and_multiply(nc, pools, ops, grouped[done], acc[done_group][:, j, :])
+                    if j == STORE_TILES - 1:
+                        finish_tiles(
+                            nc,
+                            pools,
+                            ops,
+                            (done % Q_TILES) - j,
+                            acc[done_group],
+                            row_sums[done_group],
+                            out_rows[done // Q_TILES],
+                        )
+                scores(n + AHEAD, range(1, PASSES))
+                if 1 <= n <= n_tiles:
+                    grouped[n - 1] = pools["work"].tile([P, S], BF16, name="grouped", align_bytes=64)
+                    for half in range(2):
+                        copy_half(nc, e_tr[n - 1][half], grouped[n - 1], half)
+                if n == PREPARE_NEXT_AT:
+                    batches[1] = prepare_batch(nc, pools, ident_bf, loaded[1])
+                if n < n_tiles:
+                    e_tr[n] = [transpose_half(nc, pools, ident_f32, e_sb, half) for half in range(2)]

@@ -7,6 +7,7 @@ BF16 = mybir.dt.bfloat16
 F32 = mybir.dt.float32
 U32 = mybir.dt.uint32
 U8 = mybir.dt.uint8
+I32 = mybir.dt.int32
 FP8X4 = mybir.dt.float8_e4m3fn_x4
 ALU = mybir.AluOpType
 ACT = mybir.ActivationFunctionType
@@ -22,6 +23,7 @@ BANK = 512
 BLOCKS = BANK // P
 STORE_TILES = 4
 MASKED = 1.0e30
+TENSOR_BANKS = 3
 AHEAD = 2
 PREPARE_NEXT_AT = 4
 
@@ -31,7 +33,7 @@ FLOPS = 2 * 2 * B * S * S * D
 def load_batch(nc, pools, b, q_scaled, k, v, mask):
     keep = pools["keep"]
     mask_rows = keep.tile([P, P], BF16, name="mask_rows%d" % b)
-    nc.gpsimd.memset(mask_rows[:], 0.0)
+    nc.vector.memset(mask_rows[:].bitcast(I32), 0)
     by_column = mask[b].rearrange("(ga h u e) -> u ga h e", ga=2 * PASSES, u=2, e=2)
     for u in range(2):
         rows = slice(2 * PASSES * u, 2 * PASSES * (u + 1))
@@ -47,7 +49,7 @@ def load_batch(nc, pools, b, q_scaled, k, v, mask):
     return {"b": b, "mask_rows": mask_rows, "mask_q": mask_q, "k_sb": k_sb, "q_sb": q_sb, "v_sb": v_sb}
 
 
-def prepare_batch(nc, pools, ident_bf, loaded):
+def prepare_batch(nc, pools, ident_bf, ident_f32, loaded):
     keep, psum_tr = pools["keep"], pools["psum_tr"]
     b, q_sb, k_sb, v_sb = loaded["b"], loaded["q_sb"], loaded["k_sb"], loaded["v_sb"]
 
@@ -85,6 +87,13 @@ def prepare_batch(nc, pools, ident_bf, loaded):
             nc.tensor.transpose(q_tr[:, j, :], q_sb[:, (Q_TILES // 2) * half + j, :], ident_bf[:])
         nc.scalar.copy(out=qT[:, (Q_TILES // 2) * half : (Q_TILES // 2) * (half + 1), :], in_=q_tr[:])
 
+    log_mask_rows = keep.tile([P, PASSES - TENSOR_BANKS, BANK], F32, name="log_mask_rows%d" % b)
+    for g in range(TENSOR_BANKS, PASSES):
+        rows_ps = psum_tr.tile([P, BANK], F32, tag="tr", name="rows_ps")
+        for r in range(BLOCKS):
+            nc.tensor.transpose(rows_ps[:, r * P : (r + 1) * P], log_mask[:, g * BLOCKS + r, :], ident_f32[:])
+        nc.scalar.copy(out=log_mask_rows[:, g - TENSOR_BANKS, :], in_=rows_ps[:])
+
     v_grouped = keep.tile([P, PASSES, D, PACK], BF16, name="v_grouped%d" % b, align_bytes=64)
     nc.vector.tensor_copy(out=v_grouped[:], in_=v_sb[:].rearrange("p g t d -> p g d t"))
     v_codes = keep.tile([P, PASSES * D], U32, name="v_codes%d" % b, align_bytes=64)
@@ -112,6 +121,7 @@ def prepare_batch(nc, pools, ident_bf, loaded):
         "qT": qT,
         "kT": kT,
         "log_mask": log_mask,
+        "log_mask_rows": log_mask_rows,
         "v_codes": v_codes,
         "v_scales": v_scales,
         "keep_q": keep_q,
@@ -119,7 +129,7 @@ def prepare_batch(nc, pools, ident_bf, loaded):
     }
 
 
-def score_bank(nc, pools, ident_f32, ops, t, g, neg_scores, part_min):
+def score_bank_tensor_masked(nc, pools, ident_f32, ops, t, g, neg_scores, part_min):
     s_ps = pools["psum_s"].tile([P, BANK], F32, name="s_ps")
     for r in range(BLOCKS):
         nc.tensor.matmul(
@@ -139,6 +149,19 @@ def score_bank(nc, pools, ident_f32, ops, t, g, neg_scores, part_min):
         op0=ALU.mult,
         op1=ALU.min,
         accum_out=part_min[:, g : g + 1],
+    )
+
+
+def score_bank_vector_masked(nc, pools, ops, t, g, neg_scores):
+    s_ps = pools["psum_s"].tile([P, BANK], F32, name="s_ps")
+    nc.tensor.matmul(out=s_ps[:], lhsT=ops["qT"][:, t, :], rhs=ops["kT"][:, g, :], start=True, stop=True)
+    nc.vector.scalar_tensor_tensor(
+        out=neg_scores[:, g, :],
+        in0=s_ps[:],
+        scalar=-1.0,
+        in1=ops["log_mask_rows"][:, g - TENSOR_BANKS, :],
+        op0=ALU.mult,
+        op1=ALU.subtract,
     )
 
 
@@ -172,10 +195,14 @@ def copy_half(nc, e_tr, grouped, half):
     )
 
 
-def quantise_and_multiply(nc, pools, ops, grouped, acc):
+def quantise(nc, pools, grouped):
     e_codes = pools["work"].tile([P, PASSES * P], U32, name="e_codes", align_bytes=64)
     e_scales = pools["work"].tile([P, PASSES * P], U8, name="e_scales", align_bytes=64)
     nc.vector.quantize_mx(out=e_codes[:].bitcast(FP8X4), scales=e_scales[:], in_=grouped[:])
+    return e_codes, e_scales
+
+
+def multiply(nc, ops, e_codes, e_scales, acc):
     for g in range(PASSES):
         cols = slice(g * P, (g + 1) * P)
         nc.tensor.matmul_mx(
@@ -226,27 +253,38 @@ def tile_attention_pa_kernel(tc, q_scaled, k, v, mask, out):
         make_identity(nc, ident_f32[:])
 
         loaded = [load_batch(nc, pools, b, q_scaled, k, v, mask) for b in range(B)]
-        batches = {0: prepare_batch(nc, pools, ident_bf, loaded[0])}
         out_rows = [out[b].rearrange("(p t) d -> p t d", t=Q_TILES) for b in range(B)]
 
         n_tiles = B * Q_TILES
-        neg_scores, part_min, neg_max, e_tr, grouped, row_sums, acc = {}, {}, {}, {}, {}, {}, {}
+        batches, neg_scores, part_min, neg_max, e_tr, grouped, row_sums, acc = {}, {}, {}, {}, {}, {}, {}, {}
 
-        def scores(n, banks):
+        def scores_vector_masked(n):
             if n >= n_tiles:
                 return
-            if 0 in banks:
-                neg_scores[n] = pools["scores"].tile([P, PASSES, K_PASS], F32, name="neg_scores")
-                part_min[n] = pools["small"].tile([P, PASSES], F32, name="part_min")
-            for g in banks:
-                score_bank(nc, pools, ident_f32, batches[n // Q_TILES], n % Q_TILES, g, neg_scores[n], part_min[n])
-            if PASSES - 1 in banks:
-                neg_max[n] = pools["small"].tile([P, 1], F32, name="neg_max")
-                nc.vector.tensor_reduce(out=neg_max[n][:], in_=part_min[n][:], axis=AX.X, op=ALU.min)
+            neg_scores[n] = pools["scores"].tile([P, PASSES, K_PASS], F32, name="neg_scores")
+            for g in range(TENSOR_BANKS, PASSES):
+                score_bank_vector_masked(nc, pools, batches[n // Q_TILES], n % Q_TILES, g, neg_scores[n])
+
+        def scores_tensor_masked(n):
+            if n >= n_tiles:
+                return
+            part_min[n] = pools["small"].tile([P, PASSES], F32, name="part_min")
+            for g in range(TENSOR_BANKS):
+                score_bank_tensor_masked(
+                    nc, pools, ident_f32, batches[n // Q_TILES], n % Q_TILES, g, neg_scores[n], part_min[n]
+                )
+            for g in range(TENSOR_BANKS, PASSES):
+                nc.vector.tensor_reduce(
+                    out=part_min[n][:, g : g + 1], in_=neg_scores[n][:, g, :], axis=AX.X, op=ALU.min
+                )
+            neg_max[n] = pools["small"].tile([P, 1], F32, name="neg_max")
+            nc.vector.tensor_reduce(out=neg_max[n][:], in_=part_min[n][:], axis=AX.X, op=ALU.min)
 
         with tc.manual_schedule():
+            batches[0] = prepare_batch(nc, pools, ident_bf, ident_f32, loaded[0])
             for n in range(AHEAD):
-                scores(n, range(PASSES))
+                scores_vector_masked(n)
+                scores_tensor_masked(n)
             for n in range(n_tiles + 2):
                 group = n // STORE_TILES
                 if n < n_tiles:
@@ -254,14 +292,17 @@ def tile_attention_pa_kernel(tc, q_scaled, k, v, mask, out):
                         row_sums[group] = pools["small"].tile([P, STORE_TILES], F32, name="row_sums")
                     j = n % STORE_TILES
                     e_sb = exponentials(nc, pools, neg_scores[n], neg_max[n], row_sums[group][:, j : j + 1])
-                scores(n + AHEAD, range(1))
                 done = n - 2
+                if done >= 0:
+                    e_codes, e_scales = quantise(nc, pools, grouped[done])
+                scores_vector_masked(n + AHEAD)
+                scores_tensor_masked(n + AHEAD)
                 if done >= 0:
                     done_group, j = done // STORE_TILES, done % STORE_TILES
                     ops = batches[done // Q_TILES]
                     if j == 0:
                         acc[done_group] = pools["psum_acc"].tile([P, STORE_TILES, D], F32, name="acc")
-                    quantise_and_multiply(nc, pools, ops, grouped[done], acc[done_group][:, j, :])
+                    multiply(nc, ops, e_codes, e_scales, acc[done_group][:, j, :])
                     if j == STORE_TILES - 1:
                         finish_tiles(
                             nc,
@@ -272,12 +313,11 @@ def tile_attention_pa_kernel(tc, q_scaled, k, v, mask, out):
                             row_sums[done_group],
                             out_rows[done // Q_TILES],
                         )
-                scores(n + AHEAD, range(1, PASSES))
                 if 1 <= n <= n_tiles:
                     grouped[n - 1] = pools["work"].tile([P, S], BF16, name="grouped", align_bytes=64)
                     for half in range(2):
                         copy_half(nc, e_tr[n - 1][half], grouped[n - 1], half)
                 if n == PREPARE_NEXT_AT:
-                    batches[1] = prepare_batch(nc, pools, ident_bf, loaded[1])
+                    batches[1] = prepare_batch(nc, pools, ident_bf, ident_f32, loaded[1])
                 if n < n_tiles:
                     e_tr[n] = [transpose_half(nc, pools, ident_f32, e_sb, half) for half in range(2)]

@@ -23,7 +23,6 @@ BANK = 512
 BLOCKS = BANK // P
 STORE_TILES = 4
 MASKED = 1.0e30
-TENSOR_BANKS = 3
 AHEAD = 2
 PREPARE_NEXT_AT = 4
 
@@ -49,7 +48,7 @@ def load_batch(nc, pools, b, q_scaled, k, v, mask):
     return {"b": b, "mask_rows": mask_rows, "mask_q": mask_q, "k_sb": k_sb, "q_sb": q_sb, "v_sb": v_sb}
 
 
-def prepare_batch(nc, pools, ident_bf, ident_f32, loaded):
+def prepare_batch(nc, pools, ident_bf, loaded):
     keep, psum_tr = pools["keep"], pools["psum_tr"]
     b, q_sb, k_sb, v_sb = loaded["b"], loaded["q_sb"], loaded["k_sb"], loaded["v_sb"]
 
@@ -87,13 +86,6 @@ def prepare_batch(nc, pools, ident_bf, ident_f32, loaded):
             nc.tensor.transpose(q_tr[:, j, :], q_sb[:, (Q_TILES // 2) * half + j, :], ident_bf[:])
         nc.scalar.copy(out=qT[:, (Q_TILES // 2) * half : (Q_TILES // 2) * (half + 1), :], in_=q_tr[:])
 
-    log_mask_rows = keep.tile([P, PASSES - TENSOR_BANKS, BANK], F32, name="log_mask_rows%d" % b)
-    for g in range(TENSOR_BANKS, PASSES):
-        rows_ps = psum_tr.tile([P, BANK], F32, tag="tr", name="rows_ps")
-        for r in range(BLOCKS):
-            nc.tensor.transpose(rows_ps[:, r * P : (r + 1) * P], log_mask[:, g * BLOCKS + r, :], ident_f32[:])
-        nc.scalar.copy(out=log_mask_rows[:, g - TENSOR_BANKS, :], in_=rows_ps[:])
-
     v_grouped = keep.tile([P, PASSES, D, PACK], BF16, name="v_grouped%d" % b, align_bytes=64)
     nc.vector.tensor_copy(out=v_grouped[:], in_=v_sb[:].rearrange("p g t d -> p g d t"))
     v_codes = keep.tile([P, PASSES * D], U32, name="v_codes%d" % b, align_bytes=64)
@@ -121,7 +113,6 @@ def prepare_batch(nc, pools, ident_bf, ident_f32, loaded):
         "qT": qT,
         "kT": kT,
         "log_mask": log_mask,
-        "log_mask_rows": log_mask_rows,
         "v_codes": v_codes,
         "v_scales": v_scales,
         "keep_q": keep_q,
@@ -129,7 +120,7 @@ def prepare_batch(nc, pools, ident_bf, ident_f32, loaded):
     }
 
 
-def score_bank_tensor_masked(nc, pools, ident_f32, ops, t, g, neg_scores, part_min):
+def score_bank(nc, pools, ident_f32, ops, t, g, neg_scores, part_min):
     s_ps = pools["psum_s"].tile([P, BANK], F32, name="s_ps")
     for r in range(BLOCKS):
         nc.tensor.matmul(
@@ -149,19 +140,6 @@ def score_bank_tensor_masked(nc, pools, ident_f32, ops, t, g, neg_scores, part_m
         op0=ALU.mult,
         op1=ALU.min,
         accum_out=part_min[:, g : g + 1],
-    )
-
-
-def score_bank_vector_masked(nc, pools, ops, t, g, neg_scores):
-    s_ps = pools["psum_s"].tile([P, BANK], F32, name="s_ps")
-    nc.tensor.matmul(out=s_ps[:], lhsT=ops["qT"][:, t, :], rhs=ops["kT"][:, g, :], start=True, stop=True)
-    nc.vector.scalar_tensor_tensor(
-        out=neg_scores[:, g, :],
-        in0=s_ps[:],
-        scalar=-1.0,
-        in1=ops["log_mask_rows"][:, g - TENSOR_BANKS, :],
-        op0=ALU.mult,
-        op1=ALU.subtract,
     )
 
 
@@ -258,33 +236,20 @@ def tile_attention_pa_kernel(tc, q_scaled, k, v, mask, out):
         n_tiles = B * Q_TILES
         batches, neg_scores, part_min, neg_max, e_tr, grouped, row_sums, acc = {}, {}, {}, {}, {}, {}, {}, {}
 
-        def scores_vector_masked(n):
+        def scores(n):
             if n >= n_tiles:
                 return
             neg_scores[n] = pools["scores"].tile([P, PASSES, K_PASS], F32, name="neg_scores")
-            for g in range(TENSOR_BANKS, PASSES):
-                score_bank_vector_masked(nc, pools, batches[n // Q_TILES], n % Q_TILES, g, neg_scores[n])
-
-        def scores_tensor_masked(n):
-            if n >= n_tiles:
-                return
             part_min[n] = pools["small"].tile([P, PASSES], F32, name="part_min")
-            for g in range(TENSOR_BANKS):
-                score_bank_tensor_masked(
-                    nc, pools, ident_f32, batches[n // Q_TILES], n % Q_TILES, g, neg_scores[n], part_min[n]
-                )
-            for g in range(TENSOR_BANKS, PASSES):
-                nc.vector.tensor_reduce(
-                    out=part_min[n][:, g : g + 1], in_=neg_scores[n][:, g, :], axis=AX.X, op=ALU.min
-                )
+            for g in range(PASSES):
+                score_bank(nc, pools, ident_f32, batches[n // Q_TILES], n % Q_TILES, g, neg_scores[n], part_min[n])
             neg_max[n] = pools["small"].tile([P, 1], F32, name="neg_max")
             nc.vector.tensor_reduce(out=neg_max[n][:], in_=part_min[n][:], axis=AX.X, op=ALU.min)
 
         with tc.manual_schedule():
-            batches[0] = prepare_batch(nc, pools, ident_bf, ident_f32, loaded[0])
+            batches[0] = prepare_batch(nc, pools, ident_bf, loaded[0])
             for n in range(AHEAD):
-                scores_vector_masked(n)
-                scores_tensor_masked(n)
+                scores(n)
             for n in range(n_tiles + 2):
                 group = n // STORE_TILES
                 if n < n_tiles:
@@ -295,8 +260,7 @@ def tile_attention_pa_kernel(tc, q_scaled, k, v, mask, out):
                 done = n - 2
                 if done >= 0:
                     e_codes, e_scales = quantise(nc, pools, grouped[done])
-                scores_vector_masked(n + AHEAD)
-                scores_tensor_masked(n + AHEAD)
+                scores(n + AHEAD)
                 if done >= 0:
                     done_group, j = done // STORE_TILES, done % STORE_TILES
                     ops = batches[done // Q_TILES]
@@ -318,6 +282,6 @@ def tile_attention_pa_kernel(tc, q_scaled, k, v, mask, out):
                     for half in range(2):
                         copy_half(nc, e_tr[n - 1][half], grouped[n - 1], half)
                 if n == PREPARE_NEXT_AT:
-                    batches[1] = prepare_batch(nc, pools, ident_bf, ident_f32, loaded[1])
+                    batches[1] = prepare_batch(nc, pools, ident_bf, loaded[1])
                 if n < n_tiles:
                     e_tr[n] = [transpose_half(nc, pools, ident_f32, e_sb, half) for half in range(2)]

@@ -194,12 +194,21 @@ def multiply(nc, ops, e_codes, e_scales, acc):
         )
 
 
-def finish_tiles(nc, pools, ops, first, acc, row_sums, out_rows):
-    tiles = slice(first, first + STORE_TILES)
+def reciprocal_sums(nc, pools, row_sums):
     weight = pools["small"].tile([P, STORE_TILES], F32, name="weight")
     nc.vector.reciprocal(out=weight[:], in_=row_sums[:])
+    return weight
+
+
+def keep_weights(nc, pools, ops, first, weight):
     weight_kept = pools["small"].tile([P, STORE_TILES], F32, name="weight_kept")
+    tiles = slice(first, first + STORE_TILES)
     nc.vector.tensor_tensor(out=weight_kept[:], in0=weight[:], in1=ops["keep_q"][:, tiles], op=ALU.mult)
+    return weight_kept
+
+
+def finish_tiles(nc, pools, ops, first, acc, weight_kept, out_rows):
+    tiles = slice(first, first + STORE_TILES)
     out_sb = pools["work"].tile([P, STORE_TILES, D], F32, name="out_sb")
     for j in range(STORE_TILES):
         nc.vector.scalar_tensor_tensor(
@@ -235,48 +244,67 @@ def tile_attention_pa_kernel(tc, q_scaled, k, v, mask, out):
 
         n_tiles = B * Q_TILES
         batches, neg_scores, part_min, neg_max, e_tr, grouped, row_sums, acc = {}, {}, {}, {}, {}, {}, {}, {}
+        weight, weight_kept = {}, {}
 
-        def scores(n):
+        def score_banks(n, first, last):
             if n >= n_tiles:
                 return
-            neg_scores[n] = pools["scores"].tile([P, PASSES, K_PASS], F32, name="neg_scores")
-            part_min[n] = pools["small"].tile([P, PASSES], F32, name="part_min")
-            for g in range(PASSES):
+            if first == 0:
+                neg_scores[n] = pools["scores"].tile([P, PASSES, K_PASS], F32, name="neg_scores")
+                part_min[n] = pools["small"].tile([P, PASSES], F32, name="part_min")
+            for g in range(first, last):
                 score_bank(nc, pools, ident_f32, batches[n // Q_TILES], n % Q_TILES, g, neg_scores[n], part_min[n])
+
+        def row_maximum(n):
+            if n >= n_tiles:
+                return
             neg_max[n] = pools["small"].tile([P, 1], F32, name="neg_max")
             nc.vector.tensor_reduce(out=neg_max[n][:], in_=part_min[n][:], axis=AX.X, op=ALU.min)
 
         with tc.manual_schedule():
             batches[0] = prepare_batch(nc, pools, ident_bf, loaded[0])
-            for n in range(AHEAD):
-                scores(n)
-            for n in range(n_tiles + 2):
-                group = n // STORE_TILES
+            score_banks(0, 0, PASSES)
+            score_banks(1, 0, 1)
+            row_maximum(0)
+            score_banks(1, 1, PASSES)
+            for n in range(n_tiles + 3):
                 if n < n_tiles:
-                    if n % STORE_TILES == 0:
+                    group, j = n // STORE_TILES, n % STORE_TILES
+                    if j == 0:
                         row_sums[group] = pools["small"].tile([P, STORE_TILES], F32, name="row_sums")
-                    j = n % STORE_TILES
                     e_sb = exponentials(nc, pools, neg_scores[n], neg_max[n], row_sums[group][:, j : j + 1])
                 done = n - 2
-                if done >= 0:
+                multiplies = 0 <= done < n_tiles
+                done_group, j = done // STORE_TILES, done % STORE_TILES
+                if multiplies:
                     e_codes, e_scales = quantise(nc, pools, grouped[done])
-                scores(n + AHEAD)
-                if done >= 0:
-                    done_group, j = done // STORE_TILES, done % STORE_TILES
-                    ops = batches[done // Q_TILES]
+                row_maximum(n + AHEAD - 1)
+                if done > 0 and j == 0:
+                    old = done_group - 1
+                    first = old * STORE_TILES
+                    finish_tiles(
+                        nc,
+                        pools,
+                        batches[first // Q_TILES],
+                        first % Q_TILES,
+                        acc[old],
+                        weight_kept[old],
+                        out_rows[first // Q_TILES],
+                    )
+                closes = multiplies and j == STORE_TILES - 1
+                score_banks(n + AHEAD, 0, 2)
+                if closes:
+                    weight[done_group] = reciprocal_sums(nc, pools, row_sums[done_group])
+                score_banks(n + AHEAD, 2, PASSES)
+                if closes:
+                    first = done_group * STORE_TILES
+                    weight_kept[done_group] = keep_weights(
+                        nc, pools, batches[first // Q_TILES], first % Q_TILES, weight[done_group]
+                    )
+                if multiplies:
                     if j == 0:
                         acc[done_group] = pools["psum_acc"].tile([P, STORE_TILES, D], F32, name="acc")
-                    multiply(nc, ops, e_codes, e_scales, acc[done_group][:, j, :])
-                    if j == STORE_TILES - 1:
-                        finish_tiles(
-                            nc,
-                            pools,
-                            ops,
-                            (done % Q_TILES) - j,
-                            acc[done_group],
-                            row_sums[done_group],
-                            out_rows[done // Q_TILES],
-                        )
+                    multiply(nc, batches[done // Q_TILES], e_codes, e_scales, acc[done_group][:, j, :])
                 if 1 <= n <= n_tiles:
                     grouped[n - 1] = pools["work"].tile([P, S], BF16, name="grouped", align_bytes=64)
                     for half in range(2):

@@ -24,104 +24,132 @@ BLOCKS = BANK // P
 STORE_TILES = 4
 MASKED = 1.0e30
 AHEAD = 2
-PREPARE_NEXT_AT = 4
+MASK_ROWS = S // (2 * P)
+QUARTER = Q_TILES // 4
 
 FLOPS = 2 * 2 * B * S * S * D
 
 
 def load_batch(nc, pools, b, q_scaled, k, v, mask):
     keep = pools["keep"]
-    mask_rows = keep.tile([P, P], BF16, name="mask_rows%d" % b)
-    nc.vector.memset(mask_rows[:].bitcast(I32), 0)
-    by_column = mask[b].rearrange("(ga h u e) -> u ga h e", ga=2 * PASSES, u=2, e=2)
-    for u in range(2):
-        rows = slice(2 * PASSES * u, 2 * PASSES * (u + 1))
-        nc.scalar.dma_start(out=mask_rows[rows, :].rearrange("r (h e) -> r h e", e=2), in_=by_column[u])
+    mask_raw = keep.tile([MASK_ROWS, 2 * P], BF16, name="mask_raw%d" % b)
+    nc.sync.dma_start(out=mask_raw[:], in_=mask[b].rearrange("(r c) -> r c", c=2 * P))
     mask_q = keep.tile([P, Q_TILES], BF16, name="mask_q%d" % b)
     nc.scalar.dma_start(out=mask_q[:], in_=mask[b].rearrange("(p t) -> p t", t=Q_TILES))
     k_sb = keep.tile([P, PASSES, PACK, D], BF16, name="k_sb%d" % b)
-    nc.sync.dma_start(out=k_sb[:], in_=k[b].rearrange("(g p t) d -> p g t d", g=PASSES, t=PACK))
+    k_rows = k[b].rearrange("(g p t) d -> p g t d", g=PASSES, t=PACK)
     q_sb = keep.tile([P, Q_TILES, D], BF16, name="q_sb%d" % b)
-    nc.sync.dma_start(out=q_sb[:], in_=q_scaled[b].rearrange("(p t) d -> p t d", t=Q_TILES))
+    q_rows = q_scaled[b].rearrange("(p t) d -> p t d", t=Q_TILES)
+    nc.sync.dma_start(out=k_sb[:, 0, :, :], in_=k_rows[:, 0, :, :])
+    nc.sync.dma_start(out=q_sb[:, 0:QUARTER, :], in_=q_rows[:, 0:QUARTER, :])
+    for g in range(1, PASSES):
+        nc.sync.dma_start(out=k_sb[:, g, :, :], in_=k_rows[:, g, :, :])
     v_sb = keep.tile([P, PASSES, PACK, D], BF16, name="v_sb%d" % b)
     nc.sync.dma_start(out=v_sb[:], in_=v[b].rearrange("(g p t) d -> p g t d", g=PASSES, t=PACK))
-    return {"b": b, "mask_rows": mask_rows, "mask_q": mask_q, "k_sb": k_sb, "q_sb": q_sb, "v_sb": v_sb}
+    nc.sync.dma_start(out=q_sb[:, QUARTER:Q_TILES, :], in_=q_rows[:, QUARTER:Q_TILES, :])
+    return {
+        "mask_raw": mask_raw,
+        "mask_q": mask_q,
+        "k_sb": k_sb,
+        "q_sb": q_sb,
+        "v_sb": v_sb,
+        "log_mask": keep.tile([P, S // P, P], F32, name="log_mask%d" % b),
+        "mask_lines": keep.tile([P, 2, P], BF16, name="mask_lines%d" % b),
+        "mask_col": keep.tile([P, S // P], F32, name="mask_col%d" % b),
+        "kT": keep.tile([P, PASSES, K_PASS], BF16, name="kT%d" % b),
+        "qT": keep.tile([P, Q_TILES, P], BF16, name="qT%d" % b),
+        "v_grouped": keep.tile([P, PASSES, D, PACK], BF16, name="v_grouped%d" % b, align_bytes=64),
+        "v_codes": keep.tile([P, PASSES * D], U32, name="v_codes%d" % b, align_bytes=64),
+        "v_scales": keep.tile([P, PASSES * D], U8, name="v_scales%d" % b, align_bytes=64),
+        "keep_q": keep.tile([P, Q_TILES], F32, name="keep_q%d" % b),
+        "drop_q": keep.tile([P, Q_TILES], F32, name="drop_q%d" % b),
+        "q_dropped": keep.tile([P, Q_TILES, D], BF16, name="q_dropped%d" % b),
+    }
 
 
-def prepare_batch(nc, pools, ident_bf, loaded):
-    keep, psum_tr = pools["keep"], pools["psum_tr"]
-    b, q_sb, k_sb, v_sb = loaded["b"], loaded["q_sb"], loaded["k_sb"], loaded["v_sb"]
-
-    m_tr = psum_tr.tile([P, P], BF16, tag="tr", name="m_tr")
-    nc.tensor.transpose(m_tr[:], loaded["mask_rows"][:], ident_bf[:])
-    mask_col = keep.tile([P, S // P], F32, name="mask_col%d" % b)
+def mask_columns(nc, psum, ident_bf, ops):
     nc.vector.tensor_copy(
-        out=mask_col[:].rearrange("n (g u a) -> n g u a", u=2, a=2),
-        in_=m_tr[:, 0 : S // P].rearrange("n (u g a) -> n g u a", u=2, a=2),
+        out=ops["mask_lines"][0:MASK_ROWS, :, :].rearrange("r u (h e) -> r u h e", e=2),
+        in_=ops["mask_raw"][:].rearrange("r (h u e) -> r u h e", u=2, e=2),
     )
-    log_mask = keep.tile([P, S // P, P], F32, name="log_mask%d" % b)
-    nc.gpsimd.tensor_scalar(
-        out=log_mask[:],
-        in0=mask_col[:].unsqueeze(2).to_broadcast([P, S // P, P]),
+    m_tr = psum.tile([P, 2, P], BF16, tag="bank", name="m_tr")
+    for u in range(2):
+        nc.tensor.transpose(m_tr[:, u, :], ops["mask_lines"][:, u, :], ident_bf[:])
+    nc.vector.tensor_copy(
+        out=ops["mask_col"][:].rearrange("n (g u a) -> n g u a", u=2, a=2),
+        in_=m_tr[:, :, 0:MASK_ROWS].rearrange("n u (g a) -> n g u a", a=2),
+    )
+
+
+def mask_blocks(engine, ops, g):
+    blocks = slice(BLOCKS * g, BLOCKS * (g + 1))
+    engine.tensor_scalar(
+        out=ops["log_mask"][:, blocks, :],
+        in0=ops["mask_col"][:, blocks].unsqueeze(2).to_broadcast([P, BLOCKS, P]),
         scalar1=-1.0,
         scalar2=MASKED,
         op0=ALU.add,
         op1=ALU.mult,
     )
 
-    kT = keep.tile([P, PASSES, K_PASS], BF16, name="kT%d" % b)
-    for g in range(PASSES):
-        k_tr = psum_tr.tile([P, PACK, P], BF16, tag="tr", name="k_tr")
-        for t in range(PACK):
-            nc.tensor.transpose(k_tr[:, t, :], k_sb[:, g, t, :], ident_bf[:])
-        nc.vector.tensor_copy(
-            out=kT[:, g, :].rearrange("d (u p e) -> d u p e", u=2, e=2),
-            in_=k_tr[:].rearrange("d (u e) p -> d u p e", e=2),
-        )
 
-    qT = keep.tile([P, Q_TILES, P], BF16, name="qT%d" % b)
-    for half in range(2):
-        q_tr = psum_tr.tile([P, Q_TILES // 2, P], BF16, tag="tr", name="q_tr")
-        for j in range(Q_TILES // 2):
-            nc.tensor.transpose(q_tr[:, j, :], q_sb[:, (Q_TILES // 2) * half + j, :], ident_bf[:])
-        nc.scalar.copy(out=qT[:, (Q_TILES // 2) * half : (Q_TILES // 2) * (half + 1), :], in_=q_tr[:])
-
-    v_grouped = keep.tile([P, PASSES, D, PACK], BF16, name="v_grouped%d" % b, align_bytes=64)
-    nc.vector.tensor_copy(out=v_grouped[:], in_=v_sb[:].rearrange("p g t d -> p g d t"))
-    v_codes = keep.tile([P, PASSES * D], U32, name="v_codes%d" % b, align_bytes=64)
-    v_scales = keep.tile([P, PASSES * D], U8, name="v_scales%d" % b, align_bytes=64)
-    nc.vector.quantize_mx(
-        out=v_codes[:].bitcast(FP8X4),
-        scales=v_scales[:],
-        in_=v_grouped[:].rearrange("p g d t -> p (g d t)"),
+def transpose_keys(nc, psum, ident_bf, ops, g, copy):
+    k_tr = psum.tile([P, PACK, P], BF16, tag="bank", name="k_tr")
+    for t in range(PACK):
+        nc.tensor.transpose(k_tr[:, t, :], ops["k_sb"][:, g, t, :], ident_bf[:])
+    copy(
+        out=ops["kT"][:, g, :].rearrange("d (u p e) -> d u p e", u=2, e=2),
+        in_=k_tr[:].rearrange("d (u e) p -> d u p e", e=2),
     )
 
-    keep_q = keep.tile([P, Q_TILES], F32, name="keep_q%d" % b)
-    nc.gpsimd.tensor_copy(out=keep_q[:], in_=loaded["mask_q"][:])
-    drop_q = keep.tile([P, Q_TILES], F32, name="drop_q%d" % b)
+
+def transpose_queries(nc, psum, ident_bf, ops, quarter, copy):
+    first = QUARTER * quarter
+    q_tr = psum.tile([P, QUARTER, P], BF16, tag="bank", name="q_tr")
+    for j in range(QUARTER):
+        nc.tensor.transpose(q_tr[:, j, :], ops["q_sb"][:, first + j, :], ident_bf[:])
+    copy(out=ops["qT"][:, first : first + QUARTER, :], in_=q_tr[:])
+
+
+def group_values(nc, ops, g):
     nc.gpsimd.tensor_scalar(
-        out=drop_q[:], in0=loaded["mask_q"][:], scalar1=-1.0, scalar2=1.0, op0=ALU.mult, op1=ALU.add
+        out=ops["v_grouped"][:, g, :, :],
+        in0=ops["v_sb"][:, g, :, :].rearrange("p t d -> p d t"),
+        scalar1=1.0,
+        scalar2=0.0,
+        op0=ALU.mult,
+        op1=ALU.add,
     )
-    q_dropped = keep.tile([P, Q_TILES, D], BF16, name="q_dropped%d" % b)
+
+
+def quantise_values(nc, ops, g):
+    cols = slice(g * D, (g + 1) * D)
+    nc.vector.quantize_mx(
+        out=ops["v_codes"][:, cols].bitcast(FP8X4),
+        scales=ops["v_scales"][:, cols],
+        in_=ops["v_grouped"][:, g, :, :].rearrange("p d t -> p (d t)"),
+    )
+
+
+def query_masks(nc, ops):
+    nc.gpsimd.tensor_copy(out=ops["keep_q"][:], in_=ops["mask_q"][:])
+    nc.gpsimd.tensor_scalar(
+        out=ops["drop_q"][:], in0=ops["mask_q"][:], scalar1=-1.0, scalar2=1.0, op0=ALU.mult, op1=ALU.add
+    )
+
+
+def dropped_queries(nc, ops, quarter):
+    tiles = slice(QUARTER * quarter, QUARTER * (quarter + 1))
     nc.gpsimd.tensor_tensor(
-        out=q_dropped[:],
-        in0=q_sb[:],
-        in1=drop_q[:].unsqueeze(2).to_broadcast([P, Q_TILES, D]),
+        out=ops["q_dropped"][:, tiles, :],
+        in0=ops["q_sb"][:, tiles, :],
+        in1=ops["drop_q"][:, tiles].unsqueeze(2).to_broadcast([P, QUARTER, D]),
         op=ALU.mult,
     )
-    return {
-        "qT": qT,
-        "kT": kT,
-        "log_mask": log_mask,
-        "v_codes": v_codes,
-        "v_scales": v_scales,
-        "keep_q": keep_q,
-        "q_dropped": q_dropped,
-    }
 
 
 def score_bank(nc, pools, ident_f32, ops, t, g, neg_scores, part_min):
-    s_ps = pools["psum_s"].tile([P, BANK], F32, name="s_ps")
+    s_ps = pools["psum_s"].tile([P, BANK], F32, tag="bank", name="s_ps")
     for r in range(BLOCKS):
         nc.tensor.matmul(
             out=s_ps[:, r * P : (r + 1) * P],
@@ -158,7 +186,7 @@ def exponentials(nc, pools, neg_scores, neg_max, row_sum):
 
 def transpose_half(nc, pools, ident_f32, e_sb, half):
     e_words = e_sb[:].bitcast(F32)
-    e_tr = pools["psum_tr"].tile([P, 2, 2, P], F32, tag="tr", name="e_tr")
+    e_tr = pools["psum_tr"].tile([P, 2, 2, P], F32, tag="bank", name="e_tr")
     for gg in range(2):
         for u in range(2):
             first = ((2 * half + gg) * 2 + u) * P
@@ -239,11 +267,11 @@ def tile_attention_pa_kernel(tc, q_scaled, k, v, mask, out):
         ident_f32 = pools["keep"].tile([P, P], F32, name="ident_f32")
         make_identity(nc, ident_f32[:])
 
-        loaded = [load_batch(nc, pools, b, q_scaled, k, v, mask) for b in range(B)]
+        batches = [load_batch(nc, pools, b, q_scaled, k, v, mask) for b in range(B)]
         out_rows = [out[b].rearrange("(p t) d -> p t d", t=Q_TILES) for b in range(B)]
 
         n_tiles = B * Q_TILES
-        batches, neg_scores, part_min, neg_max, e_tr, grouped, row_sums, acc = {}, {}, {}, {}, {}, {}, {}, {}
+        neg_scores, part_min, neg_max, e_tr, grouped, row_sums, acc = {}, {}, {}, {}, {}, {}, {}
         weight, weight_kept = {}, {}
 
         def score_banks(n, first, last):
@@ -262,11 +290,48 @@ def tile_attention_pa_kernel(tc, q_scaled, k, v, mask, out):
             nc.vector.tensor_reduce(out=neg_max[n][:], in_=part_min[n][:], axis=AX.X, op=ALU.min)
 
         with tc.manual_schedule():
-            batches[0] = prepare_batch(nc, pools, ident_bf, loaded[0])
-            score_banks(0, 0, PASSES)
+            start = pools["small"].tile([P, 1], F32, name="start")
+            nc.vector.memset(start[:], 0.0)
+            nc.scalar.activation(out=start[:], in_=start[:], func=ACT.Exp)
+            for ops in batches:
+                nc.vector.memset(ops["mask_lines"][:].bitcast(I32), 0)
+            psum_tr, psum_s = pools["psum_tr"], pools["psum_s"]
+            zero, one = batches
+            mask_columns(nc, psum_tr, ident_bf, zero)
+            mask_blocks(nc.vector, zero, 0)
+            for g in range(1, PASSES):
+                mask_blocks(nc.gpsimd, zero, g)
+            transpose_keys(nc, psum_tr, ident_bf, zero, 0, nc.vector.tensor_copy)
+            transpose_queries(nc, psum_tr, ident_bf, zero, 0, nc.scalar.copy)
+            for g in range(PASSES):
+                if g < PASSES - 1:
+                    transpose_keys(nc, psum_tr, ident_bf, zero, g + 1, nc.scalar.copy)
+                score_banks(0, g, g + 1)
+            for ops in batches:
+                query_masks(nc, ops)
             score_banks(1, 0, 1)
             row_maximum(0)
             score_banks(1, 1, PASSES)
+            for g in range(PASSES):
+                group_values(nc, zero, g)
+
+            bank_work = {
+                0: lambda: transpose_queries(nc, psum_s, ident_bf, zero, 1, nc.vector.tensor_copy),
+                1: lambda: mask_columns(nc, psum_s, ident_bf, one),
+                3: lambda: transpose_queries(nc, psum_s, ident_bf, zero, 2, nc.vector.tensor_copy),
+                5: lambda: transpose_queries(nc, psum_s, ident_bf, zero, 3, nc.vector.tensor_copy),
+            }
+            gpsimd_work = {}
+            value_work = {1: lambda: [quantise_values(nc, zero, g) for g in range(PASSES)]}
+            for i in range(4):
+                bank_work[6 + i] = lambda i=i: transpose_keys(nc, psum_s, ident_bf, one, i, nc.vector.tensor_copy)
+                bank_work[10 + 2 * i] = lambda i=i: transpose_queries(
+                    nc, psum_s, ident_bf, one, i, nc.vector.tensor_copy
+                )
+                gpsimd_work[1 + i] = lambda i=i: dropped_queries(nc, zero, i)
+                gpsimd_work[5 + i] = lambda i=i: (mask_blocks(nc.gpsimd, one, i), group_values(nc, one, i))
+                value_work[9 + i] = lambda i=i: quantise_values(nc, one, i)
+                gpsimd_work[10 + i] = lambda i=i: dropped_queries(nc, one, i)
             for n in range(n_tiles + 3):
                 if n < n_tiles:
                     group, j = n // STORE_TILES, n % STORE_TILES
@@ -279,6 +344,8 @@ def tile_attention_pa_kernel(tc, q_scaled, k, v, mask, out):
                 if multiplies:
                     e_codes, e_scales = quantise(nc, pools, grouped[done])
                 row_maximum(n + AHEAD - 1)
+                if n in gpsimd_work:
+                    gpsimd_work[n]()
                 if done > 0 and j == 0:
                     old = done_group - 1
                     first = old * STORE_TILES
@@ -293,6 +360,10 @@ def tile_attention_pa_kernel(tc, q_scaled, k, v, mask, out):
                     )
                 closes = multiplies and j == STORE_TILES - 1
                 score_banks(n + AHEAD, 0, 2)
+                if n in bank_work:
+                    bank_work[n]()
+                if n in value_work:
+                    value_work[n]()
                 if closes:
                     weight[done_group] = reciprocal_sums(nc, pools, row_sums[done_group])
                 score_banks(n + AHEAD, 2, PASSES)
@@ -309,7 +380,5 @@ def tile_attention_pa_kernel(tc, q_scaled, k, v, mask, out):
                     grouped[n - 1] = pools["work"].tile([P, S], BF16, name="grouped", align_bytes=64)
                     for half in range(2):
                         copy_half(nc, e_tr[n - 1][half], grouped[n - 1], half)
-                if n == PREPARE_NEXT_AT:
-                    batches[1] = prepare_batch(nc, pools, ident_bf, loaded[1])
                 if n < n_tiles:
                     e_tr[n] = [transpose_half(nc, pools, ident_f32, e_sb, half) for half in range(2)]

@@ -171,41 +171,41 @@ def score_bank(nc, pools, ident_f32, ops, t, g, neg_scores, part_min):
     )
 
 
-def exponentials(nc, pools, neg_scores, neg_max, row_sum):
-    e_sb = pools["work"].tile([P, S], BF16, name="e_sb")
+def exponentials(nc, e_sb, passes, neg_scores, neg_max, row_sum):
     nc.scalar.activation(
-        out=e_sb[:],
-        in_=neg_scores[:].rearrange("p g c -> p (g c)"),
+        out=e_sb[:, passes, :],
+        in_=neg_scores[:, passes, :],
         func=ACT.Exp,
         bias=neg_max[:],
         scale=-1.0,
         accum_out=row_sum,
     )
-    return e_sb
 
 
-def transpose_half(nc, pools, ident_f32, e_sb, half):
-    e_words = e_sb[:].bitcast(F32)
-    e_tr = pools["psum_tr"].tile([P, 2, 2, P], F32, tag="bank", name="e_tr")
-    for gg in range(2):
+def transpose_e(nc, psum, ident_f32, e_sb, passes):
+    e_words = e_sb[:].rearrange("p g c -> p (g c)").bitcast(F32)
+    e_tr = psum.tile([P, len(passes), 2, P], F32, tag="bank", name="e_tr")
+    for i, g in enumerate(passes):
         for u in range(2):
-            first = ((2 * half + gg) * 2 + u) * P
-            nc.tensor.transpose(e_tr[:, gg, u, :], e_words[:, first : first + P], ident_f32[:])
+            first = (2 * g + u) * P
+            nc.tensor.transpose(e_tr[:, i, u, :], e_words[:, first : first + P], ident_f32[:])
     return e_tr
 
 
-def copy_half(nc, e_tr, grouped, half):
+def copy_e(copy, e_tr, grouped, passes):
     grouped_words = grouped[:].bitcast(F32).rearrange("p (g i u) -> p g i u", g=PASSES, u=2)
-    nc.scalar.copy(
-        out=grouped_words[:, 2 * half : 2 * half + 2, :, :], in_=e_tr[:].rearrange("p g u i -> p g i u")
+    copy(
+        out=grouped_words[:, passes[0] : passes[-1] + 1, :, :], in_=e_tr[:].rearrange("p g u i -> p g i u")
     )
 
 
-def quantise(nc, pools, grouped):
-    e_codes = pools["work"].tile([P, PASSES * P], U32, name="e_codes", align_bytes=64)
-    e_scales = pools["work"].tile([P, PASSES * P], U8, name="e_scales", align_bytes=64)
-    nc.vector.quantize_mx(out=e_codes[:].bitcast(FP8X4), scales=e_scales[:], in_=grouped[:])
-    return e_codes, e_scales
+def quantise(nc, e_codes, e_scales, grouped, passes):
+    cols = slice(passes[0] * P, (passes[-1] + 1) * P)
+    nc.vector.quantize_mx(
+        out=e_codes[:, cols].bitcast(FP8X4),
+        scales=e_scales[:, cols],
+        in_=grouped[:, PACK * passes[0] * P : PACK * (passes[-1] + 1) * P],
+    )
 
 
 def multiply(nc, ops, e_codes, e_scales, acc):
@@ -235,10 +235,8 @@ def keep_weights(nc, pools, ops, first, weight):
     return weight_kept
 
 
-def finish_tiles(nc, pools, ops, first, acc, weight_kept, out_rows):
-    tiles = slice(first, first + STORE_TILES)
-    out_sb = pools["work"].tile([P, STORE_TILES, D], F32, name="out_sb")
-    for j in range(STORE_TILES):
+def finish_tiles(nc, out_sb, ops, first, members, acc, weight_kept, out_rows):
+    for j in members:
         nc.vector.scalar_tensor_tensor(
             out=out_sb[:, j, :],
             in0=acc[:, j, :],
@@ -247,7 +245,9 @@ def finish_tiles(nc, pools, ops, first, acc, weight_kept, out_rows):
             op0=ALU.mult,
             op1=ALU.add,
         )
-    nc.sync.dma_start(out=out_rows[:, tiles, :], in_=out_sb[:])
+    stored = slice(members[0], members[-1] + 1)
+    tiles = slice(first + members[0], first + members[-1] + 1)
+    nc.sync.dma_start(out=out_rows[:, tiles, :], in_=out_sb[:, stored, :])
 
 
 def tile_attention_pa_kernel(tc, q_scaled, k, v, mask, out):
@@ -271,8 +271,8 @@ def tile_attention_pa_kernel(tc, q_scaled, k, v, mask, out):
         out_rows = [out[b].rearrange("(p t) d -> p t d", t=Q_TILES) for b in range(B)]
 
         n_tiles = B * Q_TILES
-        neg_scores, part_min, neg_max, e_tr, grouped, row_sums, acc = {}, {}, {}, {}, {}, {}, {}
-        weight, weight_kept = {}, {}
+        neg_scores, part_min, neg_max, grouped, row_sums, acc = {}, {}, {}, {}, {}, {}
+        weight, weight_kept, out_sb = {}, {}, {}
 
         def score_banks(n, first, last):
             if n >= n_tiles:
@@ -288,6 +288,32 @@ def tile_attention_pa_kernel(tc, q_scaled, k, v, mask, out):
                 return
             neg_max[n] = pools["small"].tile([P, 1], F32, name="neg_max")
             nc.vector.tensor_reduce(out=neg_max[n][:], in_=part_min[n][:], axis=AX.X, op=ALU.min)
+
+        def code_tiles():
+            e_codes = pools["work"].tile([P, PASSES * P], U32, name="e_codes", align_bytes=64)
+            e_scales = pools["work"].tile([P, PASSES * P], U8, name="e_scales", align_bytes=64)
+            return e_codes, e_scales
+
+        def weights(group):
+            first = group * STORE_TILES
+            weight_kept[group] = keep_weights(
+                nc, pools, batches[first // Q_TILES], first % Q_TILES, weight[group]
+            )
+
+        def finish(group, members):
+            first = group * STORE_TILES
+            if members[0] == 0:
+                out_sb[group] = pools["work"].tile([P, STORE_TILES, D], F32, name="out_sb")
+            finish_tiles(
+                nc,
+                out_sb[group],
+                batches[first // Q_TILES],
+                first % Q_TILES,
+                members,
+                acc[group],
+                weight_kept[group],
+                out_rows[first // Q_TILES],
+            )
 
         with tc.manual_schedule():
             start = pools["small"].tile([P, 1], F32, name="start")
@@ -332,33 +358,33 @@ def tile_attention_pa_kernel(tc, q_scaled, k, v, mask, out):
                 gpsimd_work[5 + i] = lambda i=i: (mask_blocks(nc.gpsimd, one, i), group_values(nc, one, i))
                 value_work[9 + i] = lambda i=i: quantise_values(nc, one, i)
                 gpsimd_work[10 + i] = lambda i=i: dropped_queries(nc, one, i)
-            for n in range(n_tiles + 3):
+            halves = [range(2 * half, 2 * half + 2) for half in range(2)]
+            last = n_tiles - 1
+            for n in range(n_tiles + 1):
+                group, j = n // STORE_TILES, n % STORE_TILES
                 if n < n_tiles:
-                    group, j = n // STORE_TILES, n % STORE_TILES
                     if j == 0:
                         row_sums[group] = pools["small"].tile([P, STORE_TILES], F32, name="row_sums")
-                    e_sb = exponentials(nc, pools, neg_scores[n], neg_max[n], row_sums[group][:, j : j + 1])
+                    e_sb = pools["work"].tile([P, PASSES, K_PASS], BF16, name="e_sb")
+                    if n < last:
+                        exponentials(nc, e_sb, slice(0, PASSES), neg_scores[n], neg_max[n], row_sums[group][:, j : j + 1])
+                    else:
+                        last_sums = pools["small"].tile([P, PASSES], F32, name="last_sums")
+                        for g in range(PASSES):
+                            exponentials(
+                                nc, e_sb, slice(g, g + 1), neg_scores[n], neg_max[n], last_sums[:, g : g + 1]
+                            )
                 done = n - 2
-                multiplies = 0 <= done < n_tiles
                 done_group, j = done // STORE_TILES, done % STORE_TILES
-                if multiplies:
-                    e_codes, e_scales = quantise(nc, pools, grouped[done])
+                if done >= 0:
+                    e_codes, e_scales = code_tiles()
+                    quantise(nc, e_codes, e_scales, grouped[done], range(PASSES))
                 row_maximum(n + AHEAD - 1)
                 if n in gpsimd_work:
                     gpsimd_work[n]()
                 if done > 0 and j == 0:
-                    old = done_group - 1
-                    first = old * STORE_TILES
-                    finish_tiles(
-                        nc,
-                        pools,
-                        batches[first // Q_TILES],
-                        first % Q_TILES,
-                        acc[old],
-                        weight_kept[old],
-                        out_rows[first // Q_TILES],
-                    )
-                closes = multiplies and j == STORE_TILES - 1
+                    finish(done_group - 1, range(STORE_TILES))
+                closes = done >= 0 and j == STORE_TILES - 1
                 score_banks(n + AHEAD, 0, 2)
                 if n in bank_work:
                     bank_work[n]()
@@ -368,17 +394,33 @@ def tile_attention_pa_kernel(tc, q_scaled, k, v, mask, out):
                     weight[done_group] = reciprocal_sums(nc, pools, row_sums[done_group])
                 score_banks(n + AHEAD, 2, PASSES)
                 if closes:
-                    first = done_group * STORE_TILES
-                    weight_kept[done_group] = keep_weights(
-                        nc, pools, batches[first // Q_TILES], first % Q_TILES, weight[done_group]
-                    )
-                if multiplies:
+                    weights(done_group)
+                if done >= 0:
                     if j == 0:
                         acc[done_group] = pools["psum_acc"].tile([P, STORE_TILES, D], F32, name="acc")
                     multiply(nc, batches[done // Q_TILES], e_codes, e_scales, acc[done_group][:, j, :])
-                if 1 <= n <= n_tiles:
+                if n >= 1:
                     grouped[n - 1] = pools["work"].tile([P, S], BF16, name="grouped", align_bytes=64)
+                if 1 <= n <= last:
+                    copy = nc.scalar.copy if n < last - 1 else nc.vector.tensor_copy
                     for half in range(2):
-                        copy_half(nc, e_tr[n - 1][half], grouped[n - 1], half)
-                if n < n_tiles:
-                    e_tr[n] = [transpose_half(nc, pools, ident_f32, e_sb, half) for half in range(2)]
+                        copy_e(copy, e_tr[half], grouped[n - 1], halves[half])
+                if n < last:
+                    e_tr = [transpose_e(nc, psum_tr, ident_f32, e_sb, passes) for passes in halves]
+                elif n == last:
+                    e_tr = [transpose_e(nc, psum_s, ident_f32, e_sb, [g]) for g in range(PASSES)]
+
+            for g in range(PASSES):
+                copy_e(nc.vector.tensor_copy if g < 2 else nc.scalar.copy, e_tr[g], grouped[last], [g])
+            ops, group = batches[last // Q_TILES], last // STORE_TILES
+            nc.vector.tensor_reduce(
+                out=row_sums[group][:, STORE_TILES - 1 : STORE_TILES], in_=last_sums[:], axis=AX.X, op=ALU.add
+            )
+            e_codes, e_scales = code_tiles()
+            quantise(nc, e_codes, e_scales, grouped[last], halves[0])
+            weight[group] = reciprocal_sums(nc, pools, row_sums[group])
+            quantise(nc, e_codes, e_scales, grouped[last], halves[1])
+            weights(group)
+            multiply(nc, ops, e_codes, e_scales, acc[group][:, STORE_TILES - 1, :])
+            finish(group, range(STORE_TILES - 1))
+            finish(group, range(STORE_TILES - 1, STORE_TILES))

@@ -231,7 +231,7 @@ def reciprocal_sums(nc, pools, row_sums):
 def keep_weights(nc, pools, ops, first, weight):
     weight_kept = pools["small"].tile([P, STORE_TILES], F32, name="weight_kept")
     tiles = slice(first, first + STORE_TILES)
-    nc.vector.tensor_tensor(out=weight_kept[:], in0=weight[:], in1=ops["keep_q"][:, tiles], op=ALU.mult)
+    nc.gpsimd.tensor_tensor(out=weight_kept[:], in0=weight[:], in1=ops["keep_q"][:, tiles], op=ALU.mult)
     return weight_kept
 
 
@@ -286,8 +286,19 @@ def tile_attention_pa_kernel(tc, q_scaled, k, v, mask, out):
         def row_maximum(n):
             if n >= n_tiles:
                 return
+            first_three = pools["small"].tile([P, 1], F32, name="first_three")
+            nc.gpsimd.tensor_scalar(
+                out=first_three[:],
+                in0=part_min[n][:, 0:1],
+                scalar1=part_min[n][:, 1:2],
+                scalar2=part_min[n][:, 2:3],
+                op0=ALU.min,
+                op1=ALU.min,
+            )
             neg_max[n] = pools["small"].tile([P, 1], F32, name="neg_max")
-            nc.vector.tensor_reduce(out=neg_max[n][:], in_=part_min[n][:], axis=AX.X, op=ALU.min)
+            nc.gpsimd.tensor_scalar(
+                out=neg_max[n][:], in0=part_min[n][:, 3:4], scalar1=first_three[:], scalar2=None, op0=ALU.min
+            )
 
         def code_tiles():
             e_codes = pools["work"].tile([P, PASSES * P], U32, name="e_codes", align_bytes=64)

from contextlib import ExitStack

import concourse.mybir as mybir
from concourse.masks import make_identity

BF16 = mybir.dt.bfloat16
F32 = mybir.dt.float32
U32 = mybir.dt.uint32
U8 = mybir.dt.uint8
I32 = mybir.dt.int32
FP8X4 = mybir.dt.float8_e4m3fn_x4
ALU = mybir.AluOpType
ACT = mybir.ActivationFunctionType
AX = mybir.AxisListType

B, S, D = 2, 2048, 128
P = 128
PACK = 4
K_PASS = P * PACK
PASSES = S // K_PASS
Q_TILES = S // P
BANK = 512
BLOCKS = BANK // P
STORE_TILES = 4
MASKED = 1.0e30
AHEAD = 2
MASK_ROWS = S // (2 * P)
QUARTER = Q_TILES // 4

FLOPS = 2 * 2 * B * S * S * D


def load_batch(nc, pools, b, q_scaled, k, v, mask):
    keep = pools["keep"]
    mask_raw = keep.tile([MASK_ROWS, 2 * P], BF16, name="mask_raw%d" % b)
    nc.sync.dma_start(out=mask_raw[:], in_=mask[b].rearrange("(r c) -> r c", c=2 * P))
    mask_q = keep.tile([P, Q_TILES], BF16, name="mask_q%d" % b)
    nc.scalar.dma_start(out=mask_q[:], in_=mask[b].rearrange("(p t) -> p t", t=Q_TILES))
    k_sb = keep.tile([P, PASSES, PACK, D], BF16, name="k_sb%d" % b)
    k_rows = k[b].rearrange("(g p t) d -> p g t d", g=PASSES, t=PACK)
    q_sb = keep.tile([P, Q_TILES, D], BF16, name="q_sb%d" % b)
    q_rows = q_scaled[b].rearrange("(p t) d -> p t d", t=Q_TILES)
    nc.sync.dma_start(out=k_sb[:, 0, :, :], in_=k_rows[:, 0, :, :])
    nc.sync.dma_start(out=q_sb[:, 0:QUARTER, :], in_=q_rows[:, 0:QUARTER, :])
    for g in range(1, PASSES):
        nc.sync.dma_start(out=k_sb[:, g, :, :], in_=k_rows[:, g, :, :])
    v_sb = keep.tile([P, PASSES, PACK, D], BF16, name="v_sb%d" % b)
    nc.sync.dma_start(out=v_sb[:], in_=v[b].rearrange("(g p t) d -> p g t d", g=PASSES, t=PACK))
    nc.sync.dma_start(out=q_sb[:, QUARTER:Q_TILES, :], in_=q_rows[:, QUARTER:Q_TILES, :])
    return {
        "mask_raw": mask_raw,
        "mask_q": mask_q,
        "k_sb": k_sb,
        "q_sb": q_sb,
        "v_sb": v_sb,
        "log_mask": keep.tile([P, S // P, P], F32, name="log_mask%d" % b),
        "mask_lines": keep.tile([P, 2, P], BF16, name="mask_lines%d" % b),
        "mask_col": keep.tile([P, S // P], F32, name="mask_col%d" % b),
        "kT": keep.tile([P, PASSES, K_PASS], BF16, name="kT%d" % b),
        "qT": keep.tile([P, Q_TILES, P], BF16, name="qT%d" % b),
        "v_grouped": keep.tile([P, PASSES, D, PACK], BF16, name="v_grouped%d" % b, align_bytes=64),
        "v_codes": keep.tile([P, PASSES * D], U32, name="v_codes%d" % b, align_bytes=64),
        "v_scales": keep.tile([P, PASSES * D], U8, name="v_scales%d" % b, align_bytes=64),
        "keep_q": keep.tile([P, Q_TILES], F32, name="keep_q%d" % b),
        "drop_q": keep.tile([P, Q_TILES], F32, name="drop_q%d" % b),
        "q_dropped": keep.tile([P, Q_TILES, D], BF16, name="q_dropped%d" % b),
    }


def mask_columns(nc, psum, ident_bf, ops):
    nc.vector.tensor_copy(
        out=ops["mask_lines"][0:MASK_ROWS, :, :].rearrange("r u (h e) -> r u h e", e=2),
        in_=ops["mask_raw"][:].rearrange("r (h u e) -> r u h e", u=2, e=2),
    )
    m_tr = psum.tile([P, 2, P], BF16, tag="bank", name="m_tr")
    for u in range(2):
        nc.tensor.transpose(m_tr[:, u, :], ops["mask_lines"][:, u, :], ident_bf[:])
    nc.vector.tensor_copy(
        out=ops["mask_col"][:].rearrange("n (g u a) -> n g u a", u=2, a=2),
        in_=m_tr[:, :, 0:MASK_ROWS].rearrange("n u (g a) -> n g u a", a=2),
    )


def mask_blocks(engine, ops, g):
    blocks = slice(BLOCKS * g, BLOCKS * (g + 1))
    engine.tensor_scalar(
        out=ops["log_mask"][:, blocks, :],
        in0=ops["mask_col"][:, blocks].unsqueeze(2).to_broadcast([P, BLOCKS, P]),
        scalar1=-1.0,
        scalar2=MASKED,
        op0=ALU.add,
        op1=ALU.mult,
    )


def transpose_keys(nc, psum, ident_bf, ops, g, copy):
    k_tr = psum.tile([P, PACK, P], BF16, tag="bank", name="k_tr")
    for t in range(PACK):
        nc.tensor.transpose(k_tr[:, t, :], ops["k_sb"][:, g, t, :], ident_bf[:])
    copy(
        out=ops["kT"][:, g, :].rearrange("d (u p e) -> d u p e", u=2, e=2),
        in_=k_tr[:].rearrange("d (u e) p -> d u p e", e=2),
    )


def transpose_queries(nc, psum, ident_bf, ops, quarter, copy):
    first = QUARTER * quarter
    q_tr = psum.tile([P, QUARTER, P], BF16, tag="bank", name="q_tr")
    for j in range(QUARTER):
        nc.tensor.transpose(q_tr[:, j, :], ops["q_sb"][:, first + j, :], ident_bf[:])
    copy(out=ops["qT"][:, first : first + QUARTER, :], in_=q_tr[:])


def group_values(nc, ops, g):
    nc.gpsimd.tensor_scalar(
        out=ops["v_grouped"][:, g, :, :],
        in0=ops["v_sb"][:, g, :, :].rearrange("p t d -> p d t"),
        scalar1=1.0,
        scalar2=0.0,
        op0=ALU.mult,
        op1=ALU.add,
    )


def quantise_values(nc, ops, g):
    cols = slice(g * D, (g + 1) * D)
    nc.vector.quantize_mx(
        out=ops["v_codes"][:, cols].bitcast(FP8X4),
        scales=ops["v_scales"][:, cols],
        in_=ops["v_grouped"][:, g, :, :].rearrange("p d t -> p (d t)"),
    )


def query_masks(nc, ops):
    nc.gpsimd.tensor_copy(out=ops["keep_q"][:], in_=ops["mask_q"][:])
    nc.gpsimd.tensor_scalar(
        out=ops["drop_q"][:], in0=ops["mask_q"][:], scalar1=-1.0, scalar2=1.0, op0=ALU.mult, op1=ALU.add
    )


def dropped_queries(nc, ops, quarter):
    tiles = slice(QUARTER * quarter, QUARTER * (quarter + 1))
    nc.gpsimd.tensor_tensor(
        out=ops["q_dropped"][:, tiles, :],
        in0=ops["q_sb"][:, tiles, :],
        in1=ops["drop_q"][:, tiles].unsqueeze(2).to_broadcast([P, QUARTER, D]),
        op=ALU.mult,
    )


def score_bank(nc, pools, ident_f32, ops, t, g, neg_scores, part_min):
    s_ps = pools["psum_s"].tile([P, BANK], F32, tag="bank", name="s_ps")
    for r in range(BLOCKS):
        nc.tensor.matmul(
            out=s_ps[:, r * P : (r + 1) * P],
            lhsT=ops["log_mask"][:, g * BLOCKS + r, :],
            rhs=ident_f32[:],
            is_transpose=True,
            start=(r == 0),
            stop=False,
        )
    nc.tensor.matmul(out=s_ps[:], lhsT=ops["qT"][:, t, :], rhs=ops["kT"][:, g, :], start=False, stop=True)
    nc.vector.tensor_scalar(
        out=neg_scores[:, g, :],
        in0=s_ps[:],
        scalar1=-1.0,
        scalar2=None,
        op0=ALU.mult,
        op1=ALU.min,
        accum_out=part_min[:, g : g + 1],
    )


def exponentials(nc, e_sb, passes, neg_scores, neg_max, row_sum):
    nc.scalar.activation(
        out=e_sb[:, passes, :],
        in_=neg_scores[:, passes, :],
        func=ACT.Exp,
        bias=neg_max[:],
        scale=-1.0,
        accum_out=row_sum,
    )


def transpose_e(nc, psum, ident_f32, e_sb, passes):
    e_words = e_sb[:].rearrange("p g c -> p (g c)").bitcast(F32)
    e_tr = psum.tile([P, len(passes), 2, P], F32, tag="bank", name="e_tr")
    for i, g in enumerate(passes):
        for u in range(2):
            first = (2 * g + u) * P
            nc.tensor.transpose(e_tr[:, i, u, :], e_words[:, first : first + P], ident_f32[:])
    return e_tr


def copy_e(copy, e_tr, grouped, passes):
    grouped_words = grouped[:].bitcast(F32).rearrange("p (g i u) -> p g i u", g=PASSES, u=2)
    copy(
        out=grouped_words[:, passes[0] : passes[-1] + 1, :, :], in_=e_tr[:].rearrange("p g u i -> p g i u")
    )


def quantise(nc, e_codes, e_scales, grouped, passes):
    cols = slice(passes[0] * P, (passes[-1] + 1) * P)
    nc.vector.quantize_mx(
        out=e_codes[:, cols].bitcast(FP8X4),
        scales=e_scales[:, cols],
        in_=grouped[:, PACK * passes[0] * P : PACK * (passes[-1] + 1) * P],
    )


def multiply(nc, ops, e_codes, e_scales, acc):
    for g in range(PASSES):
        cols = slice(g * P, (g + 1) * P)
        nc.tensor.matmul_mx(
            out=acc,
            lhsT=e_codes[:, cols].bitcast(FP8X4),
            lhsT_scale=e_scales[:, cols],
            rhs=ops["v_codes"][:, cols].bitcast(FP8X4),
            rhs_scale=ops["v_scales"][:, cols],
            start=(g == 0),
            stop=(g == PASSES - 1),
        )


def reciprocal_sums(nc, pools, row_sums):
    weight = pools["small"].tile([P, STORE_TILES], F32, name="weight")
    nc.vector.reciprocal(out=weight[:], in_=row_sums[:])
    return weight


def keep_weights(nc, pools, ops, first, weight):
    weight_kept = pools["small"].tile([P, STORE_TILES], F32, name="weight_kept")
    tiles = slice(first, first + STORE_TILES)
    nc.gpsimd.tensor_tensor(out=weight_kept[:], in0=weight[:], in1=ops["keep_q"][:, tiles], op=ALU.mult)
    return weight_kept


def finish_tiles(nc, out_sb, ops, first, members, acc, weight_kept, out_rows):
    for j in members:
        nc.vector.scalar_tensor_tensor(
            out=out_sb[:, j, :],
            in0=acc[:, j, :],
            scalar=weight_kept[:, j : j + 1],
            in1=ops["q_dropped"][:, first + j, :],
            op0=ALU.mult,
            op1=ALU.add,
        )
    stored = slice(members[0], members[-1] + 1)
    tiles = slice(first + members[0], first + members[-1] + 1)
    nc.sync.dma_start(out=out_rows[:, tiles, :], in_=out_sb[:, stored, :])


def tile_attention_pa_kernel(tc, q_scaled, k, v, mask, out):
    nc = tc.nc
    with ExitStack() as ctx:
        pools = {
            "keep": ctx.enter_context(tc.tile_pool(name="keep", bufs=1)),
            "scores": ctx.enter_context(tc.tile_pool(name="scores", bufs=AHEAD + 1)),
            "work": ctx.enter_context(tc.tile_pool(name="work", bufs=2)),
            "small": ctx.enter_context(tc.tile_pool(name="small", bufs=AHEAD + 2)),
            "psum_s": ctx.enter_context(tc.psum_pool(name="psum_s", bufs=4)),
            "psum_tr": ctx.enter_context(tc.psum_pool(name="psum_tr", bufs=3)),
            "psum_acc": ctx.enter_context(tc.psum_pool(name="psum_acc", bufs=1)),
        }
        ident_bf = pools["keep"].tile([P, P], BF16, name="ident_bf")
        make_identity(nc, ident_bf[:])
        ident_f32 = pools["keep"].tile([P, P], F32, name="ident_f32")
        make_identity(nc, ident_f32[:])

        batches = [load_batch(nc, pools, b, q_scaled, k, v, mask) for b in range(B)]
        out_rows = [out[b].rearrange("(p t) d -> p t d", t=Q_TILES) for b in range(B)]

        n_tiles = B * Q_TILES
        neg_scores, part_min, neg_max, grouped, row_sums, acc = {}, {}, {}, {}, {}, {}
        weight, weight_kept, out_sb = {}, {}, {}

        def score_banks(n, first, last):
            if n >= n_tiles:
                return
            if first == 0:
                neg_scores[n] = pools["scores"].tile([P, PASSES, K_PASS], F32, name="neg_scores")
                part_min[n] = pools["small"].tile([P, PASSES], F32, name="part_min")
            for g in range(first, last):
                score_bank(nc, pools, ident_f32, batches[n // Q_TILES], n % Q_TILES, g, neg_scores[n], part_min[n])

        def row_maximum(n):
            if n >= n_tiles:
                return
            first_three = pools["small"].tile([P, 1], F32, name="first_three")
            nc.gpsimd.tensor_scalar(
                out=first_three[:],
                in0=part_min[n][:, 0:1],
                scalar1=part_min[n][:, 1:2],
                scalar2=part_min[n][:, 2:3],
                op0=ALU.min,
                op1=ALU.min,
            )
            neg_max[n] = pools["small"].tile([P, 1], F32, name="neg_max")
            nc.gpsimd.tensor_scalar(
                out=neg_max[n][:], in0=part_min[n][:, 3:4], scalar1=first_three[:], scalar2=None, op0=ALU.min
            )

        def code_tiles():
            e_codes = pools["work"].tile([P, PASSES * P], U32, name="e_codes", align_bytes=64)
            e_scales = pools["work"].tile([P, PASSES * P], U8, name="e_scales", align_bytes=64)
            return e_codes, e_scales

        def weights(group):
            first = group * STORE_TILES
            weight_kept[group] = keep_weights(
                nc, pools, batches[first // Q_TILES], first % Q_TILES, weight[group]
            )

        def finish(group, members):
            first = group * STORE_TILES
            if members[0] == 0:
                out_sb[group] = pools["work"].tile([P, STORE_TILES, D], F32, name="out_sb")
            finish_tiles(
                nc,
                out_sb[group],
                batches[first // Q_TILES],
                first % Q_TILES,
                members,
                acc[group],
                weight_kept[group],
                out_rows[first // Q_TILES],
            )

        with tc.manual_schedule():
            start = pools["small"].tile([P, 1], F32, name="start")
            nc.vector.memset(start[:], 0.0)
            nc.scalar.activation(out=start[:], in_=start[:], func=ACT.Exp)
            for ops in batches:
                nc.vector.memset(ops["mask_lines"][:].bitcast(I32), 0)
            psum_tr, psum_s = pools["psum_tr"], pools["psum_s"]
            zero, one = batches
            mask_columns(nc, psum_tr, ident_bf, zero)
            mask_blocks(nc.vector, zero, 0)
            for g in range(1, PASSES):
                mask_blocks(nc.gpsimd, zero, g)
            transpose_keys(nc, psum_tr, ident_bf, zero, 0, nc.vector.tensor_copy)
            transpose_queries(nc, psum_tr, ident_bf, zero, 0, nc.scalar.copy)
            for g in range(PASSES):
                if g < PASSES - 1:
                    transpose_keys(nc, psum_tr, ident_bf, zero, g + 1, nc.scalar.copy)
                score_banks(0, g, g + 1)
            for ops in batches:
                query_masks(nc, ops)
            score_banks(1, 0, 1)
            row_maximum(0)
            score_banks(1, 1, PASSES)
            for g in range(PASSES):
                group_values(nc, zero, g)

            bank_work = {
                0: lambda: transpose_queries(nc, psum_s, ident_bf, zero, 1, nc.vector.tensor_copy),
                1: lambda: mask_columns(nc, psum_s, ident_bf, one),
                3: lambda: transpose_queries(nc, psum_s, ident_bf, zero, 2, nc.vector.tensor_copy),
                5: lambda: transpose_queries(nc, psum_s, ident_bf, zero, 3, nc.vector.tensor_copy),
            }
            gpsimd_work = {}
            value_work = {1: lambda: [quantise_values(nc, zero, g) for g in range(PASSES)]}
            for i in range(4):
                bank_work[6 + i] = lambda i=i: transpose_keys(nc, psum_s, ident_bf, one, i, nc.vector.tensor_copy)
                bank_work[10 + 2 * i] = lambda i=i: transpose_queries(
                    nc, psum_s, ident_bf, one, i, nc.vector.tensor_copy
                )
                gpsimd_work[1 + i] = lambda i=i: dropped_queries(nc, zero, i)
                gpsimd_work[5 + i] = lambda i=i: (mask_blocks(nc.gpsimd, one, i), group_values(nc, one, i))
                value_work[9 + i] = lambda i=i: quantise_values(nc, one, i)
                gpsimd_work[10 + i] = lambda i=i: dropped_queries(nc, one, i)
            halves = [range(2 * half, 2 * half + 2) for half in range(2)]
            last = n_tiles - 1
            for n in range(n_tiles + 1):
                group, j = n // STORE_TILES, n % STORE_TILES
                if n < n_tiles:
                    if j == 0:
                        row_sums[group] = pools["small"].tile([P, STORE_TILES], F32, name="row_sums")
                    e_sb = pools["work"].tile([P, PASSES, K_PASS], BF16, name="e_sb")
                    if n < last:
                        exponentials(nc, e_sb, slice(0, PASSES), neg_scores[n], neg_max[n], row_sums[group][:, j : j + 1])
                    else:
                        last_sums = pools["small"].tile([P, PASSES], F32, name="last_sums")
                        for g in range(PASSES):
                            exponentials(
                                nc, e_sb, slice(g, g + 1), neg_scores[n], neg_max[n], last_sums[:, g : g + 1]
                            )
                done = n - 2
                done_group, j = done // STORE_TILES, done % STORE_TILES
                if done >= 0:
                    e_codes, e_scales = code_tiles()
                    quantise(nc, e_codes, e_scales, grouped[done], range(PASSES))
                row_maximum(n + AHEAD - 1)
                if n in gpsimd_work:
                    gpsimd_work[n]()
                if done > 0 and j == 0:
                    finish(done_group - 1, range(STORE_TILES))
                closes = done >= 0 and j == STORE_TILES - 1
                score_banks(n + AHEAD, 0, 2)
                if n in bank_work:
                    bank_work[n]()
                if n in value_work:
                    value_work[n]()
                if closes:
                    weight[done_group] = reciprocal_sums(nc, pools, row_sums[done_group])
                score_banks(n + AHEAD, 2, PASSES)
                if closes:
                    weights(done_group)
                if done >= 0:
                    if j == 0:
                        acc[done_group] = pools["psum_acc"].tile([P, STORE_TILES, D], F32, name="acc")
                    multiply(nc, batches[done // Q_TILES], e_codes, e_scales, acc[done_group][:, j, :])
                if n >= 1:
                    grouped[n - 1] = pools["work"].tile([P, S], BF16, name="grouped", align_bytes=64)
                if 1 <= n <= last:
                    copy = nc.scalar.copy if n < last - 1 else nc.vector.tensor_copy
                    for half in range(2):
                        copy_e(copy, e_tr[half], grouped[n - 1], halves[half])
                if n < last:
                    e_tr = [transpose_e(nc, psum_tr, ident_f32, e_sb, passes) for passes in halves]
                elif n == last:
                    e_tr = [transpose_e(nc, psum_s, ident_f32, e_sb, [g]) for g in range(PASSES)]

            for g in range(PASSES):
                copy_e(nc.vector.tensor_copy if g < 2 else nc.scalar.copy, e_tr[g], grouped[last], [g])
            ops, group = batches[last // Q_TILES], last // STORE_TILES
            nc.vector.tensor_reduce(
                out=row_sums[group][:, STORE_TILES - 1 : STORE_TILES], in_=last_sums[:], axis=AX.X, op=ALU.add
            )
            e_codes, e_scales = code_tiles()
            quantise(nc, e_codes, e_scales, grouped[last], halves[0])
            weight[group] = reciprocal_sums(nc, pools, row_sums[group])
            quantise(nc, e_codes, e_scales, grouped[last], halves[1])
            weights(group)
            multiply(nc, ops, e_codes, e_scales, acc[group][:, STORE_TILES - 1, :])
            finish(group, range(STORE_TILES - 1))
            finish(group, range(STORE_TILES - 1, STORE_TILES))
